import numpy as np
import ml_dtypes


def mxq(x, axis, fmt="e4m3"):
    dtype, down = {"e4m3": (ml_dtypes.float8_e4m3fn, 7), "e5m2": (ml_dtypes.float8_e5m2, 14)}[fmt]
    v = np.moveaxis(np.asarray(x, np.float32).astype(ml_dtypes.bfloat16).astype(np.float64), axis, -1)
    blocks = v.reshape(v.shape[:-1] + (-1, 32))
    amax = np.abs(blocks).max(-1, keepdims=True)
    byte = np.maximum(np.where(amax > 0, np.frexp(amax)[1] - 1 + 127, 0) - down, 1)
    scale = np.exp2(byte - 127.0)
    codes = (blocks / scale).astype(np.float32).astype(dtype).astype(np.float64)
    return np.moveaxis((codes * scale).reshape(v.shape), -1, axis)


WIDE = False


def mx_kscale(k):
    if not WIDE:
        return np.ones(k)
    levels = np.array([10, -10, 5, -5, 0])
    if k % 512:
        return np.exp2(np.random.permutation(np.resize(levels, k // 32))).repeat(32)
    a = np.empty((k // 512, 16))
    for p in range(k // 512):
        a[p, :8] = np.random.permutation(np.resize(levels, 8))
        for g in range(8):
            far = levels[np.abs(levels - a[p, g]) >= 10]
            a[p, g + 8] = far[np.random.randint(len(far))]
    return np.exp2(a.ravel()).repeat(32)


BF16 = ml_dtypes.bfloat16


def bf(x):
    return np.asarray(x, np.float32).astype(BF16)


def f64(x):
    return np.asarray(x).astype(np.float64)


B, S, D, E = 1, 1024, 768, 2
K = E * D


def setup_inputs():
    s = mx_kscale(K)
    return {"att": bf(np.random.standard_normal((E, B, S, D)) * 0.3 * s.reshape(E, 1, 1, D)),
            "scene_reps": bf(np.random.standard_normal((B, S, D))),
            "Wo": bf(np.random.standard_normal((D, K)) * 2.0 / np.sqrt(K) / s[None, :]),
            "bo": bf(np.random.standard_normal(D) * 0.1),
            "gamma": bf(1.0 + np.random.standard_normal(D) * 0.1),
            "beta": bf(np.random.standard_normal(D) * 0.1)}


def core(att, scene_reps, Wo, bo, gamma, beta):
    cat = np.moveaxis(f64(att), 0, 2).reshape(B, S, K)
    fused = (mxq(cat, 2, "e4m3") @ mxq(f64(Wo), 1, "e4m3").T) + f64(bo)
    y = f64(scene_reps) + fused
    mu = y.mean(-1, keepdims=True)
    var = y.var(-1, keepdims=True)
    return (y - mu) / np.sqrt(var + 1e-5) * f64(gamma) + f64(beta)


def e4m3fn_bytes(y):
    return np.clip(np.asarray(y, np.float64), -448.0, 448.0).astype(np.float32).astype(ml_dtypes.float8_e4m3fn).view(np.uint8)


def reference(att, scene_reps, Wo, bo, gamma, beta):
    out = core(att, scene_reps, Wo, bo, gamma, beta)
    s = np.max(np.abs(out)) / 448.0
    return out, e4m3fn_bytes(out / s)

@@ -1,0 +1,290 @@
+from contextlib import ExitStack
+
+import concourse.mybir as mybir
+from concourse.masks import make_identity
+
+F32 = mybir.dt.float32
+BF16 = mybir.dt.bfloat16
+U32 = mybir.dt.uint32
+U8 = mybir.dt.uint8
+FP8X4 = mybir.dt.float8_e4m3fn_x4
+FP8 = mybir.dt.float8_e4m3fn
+ALU = mybir.AluOpType
+ACT = mybir.ActivationFunctionType
+AX = mybir.AxisListType
+
+P = 128
+S = 1024
+D = 768
+E = 2
+K = E * D
+NT = S // P
+NR = D // P
+NG = K // 512
+LO = 512
+HI = D - LO
+EPS = 1e-5
+
+FLOPS = 2 * S * K * D
+
+V_BIAS_TILES = (0, 1)
+V_HI_TILES = (6, 7)
+CASTS = (("v", 0, 1536), ("s", 4096, 5120), ("v", 1536, 3072), ("s", 5120, 6144), ("v", 3072, 4096))
+
+
+def tile_heterogeneousgraphtransformer_pb_kernel(tc, att, scene_reps, Wo, bo, gamma, beta, out_0, out_1):
+    nc = tc.nc
+    att_v = att[:, 0, :, :].rearrange("e (p j) d -> j p e d", j=NT)
+    sr_v = scene_reps[0, :, :].rearrange("(p j) d -> j p d", j=NT)
+    out0_v = out_0[0, :, :].rearrange("(p j) d -> j p d", j=NT)
+    out1_v = out_1[0, :, :].rearrange("(p j) d -> p (j d)", j=NT)
+
+    with ExitStack() as ctx:
+        const = ctx.enter_context(tc.tile_pool(name="const", bufs=1))
+        keep = ctx.enter_context(tc.tile_pool(name="keep", bufs=1))
+        work = ctx.enter_context(tc.tile_pool(name="work", bufs=3))
+        ps_gb = ctx.enter_context(tc.psum_pool(name="ps_gb", bufs=1))
+        ps = ctx.enter_context(tc.psum_pool(name="ps", bufs=6))
+
+        zero_t = const.tile([P, 1], F32, name="zero_t")
+        nc.vector.memset(zero_t[:], 0.0)
+        eps_t = const.tile([P, 1], F32, name="eps_t")
+        nc.vector.tensor_scalar(out=eps_t[:], in0=zero_t[:], scalar1=EPS, scalar2=None, op0=ALU.add)
+        warm = const.tile([P, 1], F32, name="warm")
+        nc.scalar.activation(out=warm[:], in_=eps_t[:], func=ACT.Sqrt)
+
+        vecs = const.tile([P, 3, D], BF16, name="vecs")
+        nc.vector.memset(vecs[:].rearrange("p v d -> p (v d)").bitcast(F32), 0.0)
+        for i, v in enumerate((bo, gamma, beta)):
+            nc.scalar.dma_start(out=vecs[0:1, i, :], in_=v.rearrange("(o d) -> o d", o=1))
+        ones = const.tile([P, P], BF16, name="ones")
+        nc.vector.memset(ones[:], 1.0)
+        ident = const.tile([P, P], F32, name="ident")
+        make_identity(nc, ident[:])
+
+        w_raw = []
+        x_raw = []
+        sr = []
+        for r in range(NR):
+            w_raw.append(keep.tile([P, K], BF16, name="w_raw%d" % r))
+        for j in range(NT):
+            x_raw.append(keep.tile([P, K], BF16, name="x_raw%d" % j))
+            sr.append(keep.tile([P, D], BF16, name="sr%d" % j))
+
+        def load_w(r):
+            nc.sync.dma_start(out=w_raw[r][:], in_=Wo[r * P : (r + 1) * P, :])
+
+        def load_x(j):
+            nc.sync.dma_start(out=x_raw[j][:].rearrange("p (e d) -> p e d", e=E), in_=att_v[j])
+
+        def load_sr(j):
+            nc.sync.dma_start(out=sr[j][:], in_=sr_v[j])
+
+        load_x(0)
+        load_sr(0)
+        for r in range(NR):
+            load_w(r)
+        load_sr(1)
+        for j in range(1, NT):
+            load_x(j)
+        for j in range(2, NT):
+            load_sr(j)
+
+        gam_ps = ps_gb.tile([P, LO], F32, name="gam_ps")
+        bet_ps = ps_gb.tile([P, LO], F32, name="bet_ps")
+        nc.tensor.matmul(gam_ps[:], lhsT=ones[:], rhs=vecs[:, 1, 0:LO], start=True, stop=True)
+        nc.tensor.matmul(bet_ps[:], lhsT=ones[:], rhs=vecs[:, 2, 0:LO], start=True, stop=True)
+        bc1 = ps.tile([P, 512], F32, tag="bank", name="bc1")
+        bc2 = ps.tile([P, 512], F32, tag="bank", name="bc2")
+        bc3 = ps.tile([P, 512], F32, tag="bank", name="bc3")
+        nc.tensor.matmul(bc1[:], lhsT=ones[:], rhs=vecs[:, 0, 0:LO], start=True, stop=True)
+        nc.tensor.matmul(bc2[:, 0:HI], lhsT=ones[:], rhs=vecs[:, 0, LO:D], start=True, stop=True)
+        nc.tensor.matmul(bc2[:, HI : 2 * HI], lhsT=ones[:], rhs=vecs[:, 1, LO:D], start=True, stop=True)
+        nc.tensor.matmul(bc3[:, 0:HI], lhsT=ones[:], rhs=vecs[:, 2, LO:D], start=True, stop=True)
+        bo_sb = const.tile([P, D], BF16, name="bo_sb")
+        g_hi = const.tile([P, HI], F32, name="g_hi")
+        b_hi = const.tile([P, HI], F32, name="b_hi")
+        nc.scalar.copy(out=bo_sb[:, 0:LO], in_=bc1[:])
+        nc.vector.tensor_copy(out=bo_sb[:, LO:D], in_=bc2[:, 0:HI])
+        nc.vector.tensor_copy(out=g_hi[:], in_=bc2[:, HI : 2 * HI])
+        nc.scalar.copy(out=b_hi[:], in_=bc3[:, 0:HI])
+
+        gw = keep.tile([P, NG, D, 4], BF16, name="gw", align_bytes=64)
+        cw = keep.tile([P, NG, D], U32, name="cw", align_bytes=64)
+        sw = keep.tile([P, NG, D], U8, name="sw", align_bytes=64)
+        srb = []
+        cx = []
+        sx = []
+        for j in range(NT):
+            srb.append(keep.tile([P, D], F32, name="srb%d" % j))
+            cx.append(keep.tile([P, NG * P], U32, name="cx%d" % j, align_bytes=64))
+            sx.append(keep.tile([P, NG * P], U8, name="sx%d" % j, align_bytes=64))
+        o_all = keep.tile([P, NT, D], F32, name="o_all")
+        negmu = const.tile([P, NT], F32, name="negmu")
+        ssq = const.tile([P, NT], F32, name="ssq")
+        std = const.tile([P, NT], F32, name="std")
+        rstd = const.tile([P, NT], F32, name="rstd")
+        pm = const.tile([P, NT], F32, name="pm")
+
+        def turn(dst_bank, slot, words, g):
+            for u in range(2):
+                nc.tensor.transpose(dst_bank[:, slot, u, :], words[:, 256 * g + u : 256 * (g + 1) : 2], ident[:])
+
+        def weights(rp, g, eng):
+            xt = ps.tile([P, 2, 2, P], F32, tag="bank", name="xtw")
+            for tl in range(2):
+                turn(xt, tl, w_raw[2 * rp + tl][:].bitcast(F32), g)
+            dst = gw[:, g, 256 * rp : 256 * (rp + 1), :].rearrange("p c t -> p (c t)")
+            dst32 = dst.bitcast(F32).rearrange("p (t r u) -> p t r u", t=2, u=2)
+            src = xt[:].rearrange("p t u r -> p t r u")
+            if eng == "s":
+                nc.scalar.copy(out=dst32, in_=src)
+            else:
+                nc.vector.tensor_copy(out=dst32, in_=src)
+            cols = slice(256 * rp, 256 * (rp + 1))
+            nc.vector.quantize_mx(out=cw[:, g, cols].bitcast(FP8X4), scales=sw[:, g, cols], in_=dst)
+
+        gxs = {}
+
+        def turn_tokens(j):
+            words = x_raw[j][:].bitcast(F32)
+            xa = ps.tile([P, 2, 2, P], F32, tag="bank", name="xa")
+            xb = ps.tile([P, 2, 2, P], F32, tag="bank", name="xb")
+            turn(xa, 0, words, 0)
+            turn(xa, 1, words, 1)
+            turn(xb, 0, words, 2)
+            gx = keep.tile([P, NG * P * 4], BF16, name="gx%d" % j, align_bytes=64)
+            gx32 = gx[:].bitcast(F32).rearrange("p (g r u) -> p g r u", g=NG, u=2)
+            nc.scalar.copy(out=gx32[:, 0:2], in_=xa[:].rearrange("p g u r -> p g r u"))
+            nc.scalar.copy(out=gx32[:, 2:3], in_=xb[:, 0:1].rearrange("p g u r -> p g r u"))
+            gxs[j] = gx
+
+        def quantise_tokens(j):
+            gx = gxs[j]
+            nc.vector.quantize_mx(out=cx[j][:, 0:256].bitcast(FP8X4), scales=sx[j][:, 0:256], in_=gx[:, 0:1024])
+            nc.vector.quantize_mx(out=cx[j][:, 256:384].bitcast(FP8X4), scales=sx[j][:, 256:384], in_=gx[:, 1024:1536])
+
+        def add_bias(j):
+            eng = nc.vector if j in V_BIAS_TILES else nc.gpsimd
+            eng.tensor_tensor(out=srb[j][:], in0=sr[j][:], in1=bo_sb[:], op=ALU.add)
+
+        accs = {}
+
+        def multiply(j):
+            acc_lo = ps.tile([P, 512], F32, tag="bank", name="acc_lo")
+            acc_hi = ps.tile([P, 512], F32, tag="bank", name="acc_hi")
+            for g in range(NG):
+                tok = slice(g * P, (g + 1) * P)
+                for acc, c0, c1 in ((acc_lo[:, 0:LO], 0, LO), (acc_hi[:, 0:HI], LO, D)):
+                    nc.tensor.matmul_mx(
+                        out=acc,
+                        lhsT=cx[j][:, tok].bitcast(FP8X4),
+                        lhsT_scale=sx[j][:, tok],
+                        rhs=cw[:, g, c0:c1].bitcast(FP8X4),
+                        rhs_scale=sw[:, g, c0:c1],
+                        start=(g == 0),
+                        stop=(g == NG - 1),
+                    )
+            accs[j] = (acc_lo, acc_hi)
+
+        ys = {}
+
+        def residual_and_stats(j):
+            acc_lo, acc_hi = accs[j]
+            y = work.tile([P, D], F32, tag="y", name="y", bufs=4)
+            nc.vector.tensor_tensor(out=y[:, 0:LO], in0=acc_lo[:, 0:LO], in1=srb[j][:, 0:LO], op=ALU.add)
+            nc.vector.tensor_tensor(out=y[:, LO:D], in0=acc_hi[:, 0:HI], in1=srb[j][:, LO:D], op=ALU.add)
+            col = slice(j, j + 1)
+            junk = work.tile([P, D], BF16, tag="junk", name="junk", bufs=2)
+            nc.scalar.activation(out=junk[:], in_=y[:], func=ACT.Identity, scale=-1.0 / D, accum_out=negmu[:, col])
+            junk2 = work.tile([P, D], BF16, tag="junk", name="junk2", bufs=2)
+            nc.scalar.activation(out=junk2[:], in_=y[:], func=ACT.Square, bias=negmu[:, col], accum_out=ssq[:, col])
+            nc.scalar.activation(out=std[:, col], in_=ssq[:, col], func=ACT.Sqrt, bias=eps_t[:, 0:1], scale=1.0 / D)
+            ys[j] = y
+
+        def normalise(j):
+            y = ys[j]
+            col = slice(j, j + 1)
+            last = j in V_HI_TILES
+            t = work.tile([P, D], F32, tag="t", name="t", bufs=3)
+            nc.vector.scalar_tensor_tensor(
+                out=t[:, 0:LO], in0=y[:, 0:LO], scalar=negmu[:, col], in1=gam_ps[:], op0=ALU.add, op1=ALU.mult
+            )
+            if last:
+                nc.vector.scalar_tensor_tensor(
+                    out=t[:, LO:D], in0=y[:, LO:D], scalar=negmu[:, col], in1=g_hi[:], op0=ALU.add, op1=ALU.mult
+                )
+            nc.vector.reciprocal(out=rstd[:, col], in_=std[:, col])
+            nc.vector.scalar_tensor_tensor(
+                out=o_all[:, j, 0:LO], in0=t[:, 0:LO], scalar=rstd[:, col], in1=bet_ps[:], op0=ALU.mult, op1=ALU.add
+            )
+            if last:
+                nc.vector.scalar_tensor_tensor(
+                    out=o_all[:, j, LO:D], in0=t[:, LO:D], scalar=rstd[:, col], in1=b_hi[:], op0=ALU.mult, op1=ALU.add
+                )
+            else:
+                z = work.tile([P, HI], F32, tag="z", name="z", bufs=3)
+                nc.gpsimd.tensor_scalar(
+                    out=z[:], in0=y[:, LO:D], scalar1=negmu[:, col], scalar2=rstd[:, col], op0=ALU.add, op1=ALU.mult
+                )
+                nc.gpsimd.tensor_tensor(out=z[:], in0=z[:], in1=g_hi[:], op=ALU.mult)
+                nc.gpsimd.tensor_tensor(out=o_all[:, j, LO:D], in0=z[:], in1=b_hi[:], op=ALU.add)
+
+        def amax_and_store(j):
+            nc.vector.tensor_reduce(
+                out=pm[:, j : j + 1], in_=o_all[:, j, :], axis=AX.X, op=ALU.max, apply_absolute_value=True
+            )
+            nc.sync.dma_start(out=out0_v[j], in_=o_all[:, j, :])
+
+        turn_tokens(0)
+        quantise_tokens(0)
+        add_bias(0)
+        n = 0
+        for rp in range(NR // 2):
+            for g in range(NG):
+                weights(rp, g, "s" if n % 2 == 0 else "v")
+                n += 1
+        add_bias(1)
+        multiply(0)
+        for j in range(1, NT):
+            turn_tokens(j)
+            quantise_tokens(j)
+            if j == 3:
+                multiply(1)
+            if j == 6:
+                multiply(2)
+
+        for j in range(NT):
+            if 3 <= j + 2 < NT:
+                multiply(j + 2)
+            if 2 <= j + 2 < NT:
+                add_bias(j + 2)
+            residual_and_stats(j)
+            normalise(j)
+            if j >= 1:
+                amax_and_store(j - 1)
+        amax_and_store(NT - 1)
+
+        pmax = const.tile([P, 1], F32, name="pmax")
+        nc.vector.tensor_reduce(out=pmax[:], in_=pm[:], axis=AX.X, op=ALU.max)
+        tp = ps.tile([P, 512], F32, tag="bank", name="tp")
+        nc.tensor.transpose(tp[:, 0:P], pmax[:, 0:1].to_broadcast([P, P]), ident[:])
+        amax = const.tile([P, 1], F32, name="amax")
+        nc.vector.tensor_reduce(out=amax[:], in_=tp[:, 0:P], axis=AX.X, op=ALU.max)
+        rec = const.tile([P, 1], F32, name="rec")
+        nc.vector.reciprocal(out=rec[:], in_=amax[:])
+        fac = const.tile([P, 1], F32, name="fac")
+        nc.vector.tensor_scalar(out=fac[:], in0=rec[:], scalar1=448.0, scalar2=None, op0=ALU.mult)
+
+        o_flat = o_all[:].rearrange("p j d -> p (j d)")
+        for i, (eng, c0, c1) in enumerate(CASTS):
+            q = keep.tile([P, c1 - c0], FP8, name="q%d" % i)
+            if eng == "v":
+                nc.vector.tensor_scalar(
+                    out=q[:], in0=o_flat[:, c0:c1], scalar1=fac[:, 0:1], scalar2=None, op0=ALU.mult, saturate=False
+                )
+            else:
+                nc.scalar.activation(
+                    out=q[:], in_=o_flat[:, c0:c1], func=ACT.Identity, scale=fac[:, 0:1], bias=zero_t[:, 0:1], saturate=False
+                )
+            nc.sync.dma_start(out=out1_v[:, c0:c1], in_=q[:].bitcast(U8))

@@ -19,7 +19,8 @@ D = 768
 E = 2
 K = E * D
 NT = S // P
-NR = D // P
+NC = 3
+CW = D // NC
 NG = K // 512
 LO = 512
 HI = D - LO
@@ -27,8 +28,13 @@ EPS = 1e-5
 
 FLOPS = 2 * S * K * D
 
-V_BIAS_TILES = (0, 1)
-V_HI_TILES = (6, 7)
+V_BIAS_TILES = ()
+V_HI_TILES = (7,)
+V_WEIGHT_BANKS = (1, 4, 7)
+LOADS = (("s", 1), ("x", 1), ("x", 2), ("s", 2), ("x", 3), ("x", 4), ("s", 3), ("x", 5), ("x", 6), ("s", 4), ("x", 7), ("s", 5), ("s", 6), ("s", 7))
+GROUPS = ((0,), (1,), (2,), (3, 4), (5, 6), (7,))
+PREFETCH = (3, 4, 5)
+AMAX = {2: (0, 2), 4: (2, 4), 6: (4, 6), 7: (6, 7), 8: (7, 8)}
 CASTS = (("v", 0, 1536), ("s", 4096, 5120), ("v", 1536, 3072), ("s", 5120, 6144), ("v", 3072, 4096))
 
 
@@ -51,7 +57,7 @@ def tile_heterogeneousgraphtransformer_pb_kernel(tc, att, scene_reps, Wo, bo, ga
         eps_t = const.tile([P, 1], F32, name="eps_t")
         nc.vector.tensor_scalar(out=eps_t[:], in0=zero_t[:], scalar1=EPS, scalar2=None, op0=ALU.add)
         warm = const.tile([P, 1], F32, name="warm")
-        nc.scalar.activation(out=warm[:], in_=eps_t[:], func=ACT.Sqrt)
+        nc.scalar.activation(out=warm[:], in_=eps_t[:], func=ACT.Abs_reciprocal_sqrt)
 
         vecs = const.tile([P, 3, D], BF16, name="vecs")
         nc.vector.memset(vecs[:].rearrange("p v d -> p (v d)").bitcast(F32), 0.0)
@@ -65,14 +71,11 @@ def tile_heterogeneousgraphtransformer_pb_kernel(tc, att, scene_reps, Wo, bo, ga
         w_raw = []
         x_raw = []
         sr = []
-        for r in range(NR):
+        for r in range(2 * NC):
             w_raw.append(keep.tile([P, K], BF16, name="w_raw%d" % r))
         for j in range(NT):
             x_raw.append(keep.tile([P, K], BF16, name="x_raw%d" % j))
             sr.append(keep.tile([P, D], BF16, name="sr%d" % j))
-
-        def load_w(r):
-            nc.sync.dma_start(out=w_raw[r][:], in_=Wo[r * P : (r + 1) * P, :])
 
         def load_x(j):
             nc.sync.dma_start(out=x_raw[j][:].rearrange("p (e d) -> p e d", e=E), in_=att_v[j])
@@ -82,18 +85,19 @@ def tile_heterogeneousgraphtransformer_pb_kernel(tc, att, scene_reps, Wo, bo, ga
 
         load_x(0)
         load_sr(0)
-        for r in range(NR):
-            load_w(r)
-        load_sr(1)
-        for j in range(1, NT):
-            load_x(j)
-        for j in range(2, NT):
-            load_sr(j)
+        for r in range(2 * NC):
+            nc.sync.dma_start(out=w_raw[r][:], in_=Wo[r * P : (r + 1) * P, :])
+        for what, j in LOADS:
+            if what == "x":
+                load_x(j)
+            else:
+                load_sr(j)
 
         gam_ps = ps_gb.tile([P, LO], F32, name="gam_ps")
         bet_ps = ps_gb.tile([P, LO], F32, name="bet_ps")
-        nc.tensor.matmul(gam_ps[:], lhsT=ones[:], rhs=vecs[:, 1, 0:LO], start=True, stop=True)
-        nc.tensor.matmul(bet_ps[:], lhsT=ones[:], rhs=vecs[:, 2, 0:LO], start=True, stop=True)
+        bo_sb = const.tile([P, D], BF16, name="bo_sb")
+        g_hi = const.tile([P, HI], F32, name="g_hi")
+        b_hi = const.tile([P, HI], F32, name="b_hi")
         bc1 = ps.tile([P, 512], F32, tag="bank", name="bc1")
         bc2 = ps.tile([P, 512], F32, tag="bank", name="bc2")
         bc3 = ps.tile([P, 512], F32, tag="bank", name="bc3")
@@ -101,28 +105,19 @@ def tile_heterogeneousgraphtransformer_pb_kernel(tc, att, scene_reps, Wo, bo, ga
         nc.tensor.matmul(bc2[:, 0:HI], lhsT=ones[:], rhs=vecs[:, 0, LO:D], start=True, stop=True)
         nc.tensor.matmul(bc2[:, HI : 2 * HI], lhsT=ones[:], rhs=vecs[:, 1, LO:D], start=True, stop=True)
         nc.tensor.matmul(bc3[:, 0:HI], lhsT=ones[:], rhs=vecs[:, 2, LO:D], start=True, stop=True)
-        bo_sb = const.tile([P, D], BF16, name="bo_sb")
-        g_hi = const.tile([P, HI], F32, name="g_hi")
-        b_hi = const.tile([P, HI], F32, name="b_hi")
+        nc.tensor.matmul(gam_ps[:], lhsT=ones[:], rhs=vecs[:, 1, 0:LO], start=True, stop=True)
+        nc.tensor.matmul(bet_ps[:], lhsT=ones[:], rhs=vecs[:, 2, 0:LO], start=True, stop=True)
         nc.scalar.copy(out=bo_sb[:, 0:LO], in_=bc1[:])
-        nc.vector.tensor_copy(out=bo_sb[:, LO:D], in_=bc2[:, 0:HI])
-        nc.vector.tensor_copy(out=g_hi[:], in_=bc2[:, HI : 2 * HI])
+        nc.scalar.copy(out=bo_sb[:, LO:D], in_=bc2[:, 0:HI])
+        nc.scalar.copy(out=g_hi[:], in_=bc2[:, HI : 2 * HI])
         nc.scalar.copy(out=b_hi[:], in_=bc3[:, 0:HI])
 
-        gw = keep.tile([P, NG, D, 4], BF16, name="gw", align_bytes=64)
-        cw = keep.tile([P, NG, D], U32, name="cw", align_bytes=64)
-        sw = keep.tile([P, NG, D], U8, name="sw", align_bytes=64)
         srb = []
-        cx = []
-        sx = []
         for j in range(NT):
             srb.append(keep.tile([P, D], F32, name="srb%d" % j))
-            cx.append(keep.tile([P, NG * P], U32, name="cx%d" % j, align_bytes=64))
-            sx.append(keep.tile([P, NG * P], U8, name="sx%d" % j, align_bytes=64))
         o_all = keep.tile([P, NT, D], F32, name="o_all")
         negmu = const.tile([P, NT], F32, name="negmu")
         ssq = const.tile([P, NT], F32, name="ssq")
-        std = const.tile([P, NT], F32, name="std")
         rstd = const.tile([P, NT], F32, name="rstd")
         pm = const.tile([P, NT], F32, name="pm")
 
@@ -130,58 +125,93 @@ def tile_heterogeneousgraphtransformer_pb_kernel(tc, att, scene_reps, Wo, bo, ga
             for u in range(2):
                 nc.tensor.transpose(dst_bank[:, slot, u, :], words[:, 256 * g + u : 256 * (g + 1) : 2], ident[:])
 
-        def weights(rp, g, eng):
-            xt = ps.tile([P, 2, 2, P], F32, tag="bank", name="xtw")
-            for tl in range(2):
-                turn(xt, tl, w_raw[2 * rp + tl][:].bitcast(F32), g)
-            dst = gw[:, g, 256 * rp : 256 * (rp + 1), :].rearrange("p c t -> p (c t)")
-            dst32 = dst.bitcast(F32).rearrange("p (t r u) -> p t r u", t=2, u=2)
-            src = xt[:].rearrange("p t u r -> p t r u")
+        def empty(eng, dst32, bank_view):
             if eng == "s":
-                nc.scalar.copy(out=dst32, in_=src)
+                nc.scalar.copy(out=dst32, in_=bank_view)
             else:
-                nc.vector.tensor_copy(out=dst32, in_=src)
-            cols = slice(256 * rp, 256 * (rp + 1))
-            nc.vector.quantize_mx(out=cw[:, g, cols].bitcast(FP8X4), scales=sw[:, g, cols], in_=dst)
+                nc.vector.tensor_copy(out=dst32, in_=bank_view)
 
-        gxs = {}
+        def pair_to_codes(raws, name, engs):
+            banks = []
+            for g in range(NG):
+                banks.append(ps.tile([P, 2, 2, P], F32, tag="bank", name="xt_%s_%d" % (name, g)))
+            for tl in range(2):
+                for g in range(NG):
+                    turn(banks[g], tl, raws[tl][:].bitcast(F32), g)
+            grouped = keep.tile([P, NG * 1024], BF16, name="grp_" + name, align_bytes=64)
+            g32 = grouped[:].bitcast(F32).rearrange("p (g t r u) -> p g t r u", g=NG, t=2, u=2)
+            for g in range(NG):
+                empty(engs[g], g32[:, g], banks[g][:].rearrange("p t u r -> p t r u"))
+            return grouped
 
-        def turn_tokens(j):
-            words = x_raw[j][:].bitcast(F32)
-            xa = ps.tile([P, 2, 2, P], F32, tag="bank", name="xa")
-            xb = ps.tile([P, 2, 2, P], F32, tag="bank", name="xb")
+        def quantise_pair(grouped, name):
+            codes = keep.tile([P, NG * 256], U32, name="c_" + name, align_bytes=64)
+            scales = keep.tile([P, NG * 256], U8, name="s_" + name, align_bytes=64)
+            nc.vector.quantize_mx(out=codes[:, 0:512].bitcast(FP8X4), scales=scales[:, 0:512], in_=grouped[:, 0:2048])
+            nc.vector.quantize_mx(out=codes[:, 512:768].bitcast(FP8X4), scales=scales[:, 512:768], in_=grouped[:, 2048:3072])
+            return codes, scales
+
+        def single_to_codes(raw, name):
+            words = raw[:].bitcast(F32)
+            xa = ps.tile([P, 2, 2, P], F32, tag="bank", name="xa_" + name)
+            xb = ps.tile([P, 2, 2, P], F32, tag="bank", name="xb_" + name)
             turn(xa, 0, words, 0)
             turn(xa, 1, words, 1)
             turn(xb, 0, words, 2)
-            gx = keep.tile([P, NG * P * 4], BF16, name="gx%d" % j, align_bytes=64)
-            gx32 = gx[:].bitcast(F32).rearrange("p (g r u) -> p g r u", g=NG, u=2)
-            nc.scalar.copy(out=gx32[:, 0:2], in_=xa[:].rearrange("p g u r -> p g r u"))
-            nc.scalar.copy(out=gx32[:, 2:3], in_=xb[:, 0:1].rearrange("p g u r -> p g r u"))
-            gxs[j] = gx
+            grouped = keep.tile([P, NG * 512], BF16, name="grp_" + name, align_bytes=64)
+            g32 = grouped[:].bitcast(F32).rearrange("p (g r u) -> p g r u", g=NG, u=2)
+            nc.scalar.copy(out=g32[:, 0:2], in_=xa[:].rearrange("p g u r -> p g r u"))
+            nc.scalar.copy(out=g32[:, 2:3], in_=xb[:, 0:1].rearrange("p g u r -> p g r u"))
+            return grouped
 
-        def quantise_tokens(j):
-            gx = gxs[j]
-            nc.vector.quantize_mx(out=cx[j][:, 0:256].bitcast(FP8X4), scales=sx[j][:, 0:256], in_=gx[:, 0:1024])
-            nc.vector.quantize_mx(out=cx[j][:, 256:384].bitcast(FP8X4), scales=sx[j][:, 256:384], in_=gx[:, 1024:1536])
+        def quantise_single(grouped, name):
+            codes = keep.tile([P, NG * P], U32, name="c_" + name, align_bytes=64)
+            scales = keep.tile([P, NG * P], U8, name="s_" + name, align_bytes=64)
+            nc.vector.quantize_mx(out=codes[:, 0:256].bitcast(FP8X4), scales=scales[:, 0:256], in_=grouped[:, 0:1024])
+            nc.vector.quantize_mx(out=codes[:, 256:384].bitcast(FP8X4), scales=scales[:, 256:384], in_=grouped[:, 1024:1536])
+            return codes, scales
+
+        grouped_of = {}
+        tok = {}
+
+        def turn_group(n):
+            grp = GROUPS[n]
+            if len(grp) == 1:
+                grouped_of[n] = single_to_codes(x_raw[grp[0]], "x%d" % n)
+            else:
+                grouped_of[n] = pair_to_codes([x_raw[grp[0]], x_raw[grp[1]]], "x%d" % n, "sss")
+
+        def quantise_group(n):
+            grp = GROUPS[n]
+            if len(grp) == 1:
+                codes, scales = quantise_single(grouped_of[n], "x%d" % n)
+                tok[grp[0]] = (codes, scales, 0, P)
+            else:
+                codes, scales = quantise_pair(grouped_of[n], "x%d" % n)
+                tok[grp[0]] = (codes, scales, 0, 2 * P)
+                tok[grp[1]] = (codes, scales, P, 2 * P)
 
         def add_bias(j):
             eng = nc.vector if j in V_BIAS_TILES else nc.gpsimd
             eng.tensor_tensor(out=srb[j][:], in0=sr[j][:], in1=bo_sb[:], op=ALU.add)
 
+        wq = []
         accs = {}
 
         def multiply(j):
+            codes, scales, first, step = tok[j]
             acc_lo = ps.tile([P, 512], F32, tag="bank", name="acc_lo")
             acc_hi = ps.tile([P, 512], F32, tag="bank", name="acc_hi")
-            for g in range(NG):
-                tok = slice(g * P, (g + 1) * P)
-                for acc, c0, c1 in ((acc_lo[:, 0:LO], 0, LO), (acc_hi[:, 0:HI], LO, D)):
+            outs = (acc_lo[:, 0:CW], acc_lo[:, CW : 2 * CW], acc_hi[:, 0:CW])
+            for c in range(NC):
+                for g in range(NG):
+                    cols = slice(first + g * step, first + g * step + P)
                     nc.tensor.matmul_mx(
-                        out=acc,
-                        lhsT=cx[j][:, tok].bitcast(FP8X4),
-                        lhsT_scale=sx[j][:, tok],
-                        rhs=cw[:, g, c0:c1].bitcast(FP8X4),
-                        rhs_scale=sw[:, g, c0:c1],
+                        out=outs[c],
+                        lhsT=codes[:, cols].bitcast(FP8X4),
+                        lhsT_scale=scales[:, cols],
+                        rhs=wq[c][0][:, g * CW : (g + 1) * CW].bitcast(FP8X4),
+                        rhs_scale=wq[c][1][:, g * CW : (g + 1) * CW],
                         start=(g == 0),
                         stop=(g == NG - 1),
                     )
@@ -199,26 +229,34 @@ def tile_heterogeneousgraphtransformer_pb_kernel(tc, att, scene_reps, Wo, bo, ga
             nc.scalar.activation(out=junk[:], in_=y[:], func=ACT.Identity, scale=-1.0 / D, accum_out=negmu[:, col])
             junk2 = work.tile([P, D], BF16, tag="junk", name="junk2", bufs=2)
             nc.scalar.activation(out=junk2[:], in_=y[:], func=ACT.Square, bias=negmu[:, col], accum_out=ssq[:, col])
-            nc.scalar.activation(out=std[:, col], in_=ssq[:, col], func=ACT.Sqrt, bias=eps_t[:, 0:1], scale=1.0 / D)
+            nc.scalar.activation(
+                out=rstd[:, col], in_=ssq[:, col], func=ACT.Abs_reciprocal_sqrt, bias=eps_t[:, 0:1], scale=1.0 / D
+            )
             ys[j] = y
 
-        def normalise(j):
+        ts = {}
+
+        def centre(j):
             y = ys[j]
             col = slice(j, j + 1)
-            last = j in V_HI_TILES
             t = work.tile([P, D], F32, tag="t", name="t", bufs=3)
+            ts[j] = t
             nc.vector.scalar_tensor_tensor(
                 out=t[:, 0:LO], in0=y[:, 0:LO], scalar=negmu[:, col], in1=gam_ps[:], op0=ALU.add, op1=ALU.mult
             )
-            if last:
+            if j in V_HI_TILES:
                 nc.vector.scalar_tensor_tensor(
                     out=t[:, LO:D], in0=y[:, LO:D], scalar=negmu[:, col], in1=g_hi[:], op0=ALU.add, op1=ALU.mult
                 )
-            nc.vector.reciprocal(out=rstd[:, col], in_=std[:, col])
+
+        def scale_shift(j):
+            y = ys[j]
+            t = ts[j]
+            col = slice(j, j + 1)
             nc.vector.scalar_tensor_tensor(
                 out=o_all[:, j, 0:LO], in0=t[:, 0:LO], scalar=rstd[:, col], in1=bet_ps[:], op0=ALU.mult, op1=ALU.add
             )
-            if last:
+            if j in V_HI_TILES:
                 nc.vector.scalar_tensor_tensor(
                     out=o_all[:, j, LO:D], in0=t[:, LO:D], scalar=rstd[:, col], in1=b_hi[:], op0=ALU.mult, op1=ALU.add
                 )
@@ -230,49 +268,61 @@ def tile_heterogeneousgraphtransformer_pb_kernel(tc, att, scene_reps, Wo, bo, ga
                 nc.gpsimd.tensor_tensor(out=z[:], in0=z[:], in1=g_hi[:], op=ALU.mult)
                 nc.gpsimd.tensor_tensor(out=o_all[:, j, LO:D], in0=z[:], in1=b_hi[:], op=ALU.add)
 
-        def amax_and_store(j):
+        def amax(j0, j1):
             nc.vector.tensor_reduce(
-                out=pm[:, j : j + 1], in_=o_all[:, j, :], axis=AX.X, op=ALU.max, apply_absolute_value=True
+                out=pm[:, j0:j1], in_=o_all[:, j0:j1, :], axis=AX.X, op=ALU.max, apply_absolute_value=True
             )
+
+        def store(j):
             nc.sync.dma_start(out=out0_v[j], in_=o_all[:, j, :])
 
-        turn_tokens(0)
-        quantise_tokens(0)
+        turn_group(0)
+        quantise_group(0)
         add_bias(0)
-        n = 0
-        for rp in range(NR // 2):
+        for c in range(NC):
+            engs = ""
             for g in range(NG):
-                weights(rp, g, "s" if n % 2 == 0 else "v")
-                n += 1
+                engs += "v" if (c * NG + g) in V_WEIGHT_BANKS else "s"
+            grouped = pair_to_codes([w_raw[2 * c], w_raw[2 * c + 1]], "w%d" % c, engs)
+            wq.append(quantise_pair(grouped, "w%d" % c))
         add_bias(1)
         multiply(0)
-        for j in range(1, NT):
-            turn_tokens(j)
-            quantise_tokens(j)
-            if j == 3:
-                multiply(1)
-            if j == 6:
-                multiply(2)
+        turn_group(1)
+        quantise_group(1)
+        residual_and_stats(0)
+        multiply(1)
+        turn_group(2)
+        quantise_group(2)
+        add_bias(2)
 
-        for j in range(NT):
-            if 3 <= j + 2 < NT:
-                multiply(j + 2)
-            if 2 <= j + 2 < NT:
-                add_bias(j + 2)
-            residual_and_stats(j)
-            normalise(j)
-            if j >= 1:
-                amax_and_store(j - 1)
-        amax_and_store(NT - 1)
+        for i in range(NT + 1):
+            if i + 2 < NT:
+                multiply(i + 2)
+            if i < len(PREFETCH):
+                turn_group(PREFETCH[i])
+            if i + 1 < NT:
+                residual_and_stats(i + 1)
+            if i < NT:
+                centre(i)
+            if i in AMAX:
+                amax(AMAX[i][0], AMAX[i][1])
+            if i >= 1:
+                store(i - 1)
+            if i < NT:
+                scale_shift(i)
+            if i + 3 < NT:
+                add_bias(i + 3)
+            if i < len(PREFETCH):
+                quantise_group(PREFETCH[i])
 
         pmax = const.tile([P, 1], F32, name="pmax")
         nc.vector.tensor_reduce(out=pmax[:], in_=pm[:], axis=AX.X, op=ALU.max)
         tp = ps.tile([P, 512], F32, tag="bank", name="tp")
         nc.tensor.transpose(tp[:, 0:P], pmax[:, 0:1].to_broadcast([P, P]), ident[:])
-        amax = const.tile([P, 1], F32, name="amax")
-        nc.vector.tensor_reduce(out=amax[:], in_=tp[:, 0:P], axis=AX.X, op=ALU.max)
+        amax_t = const.tile([P, 1], F32, name="amax_t")
+        nc.vector.tensor_reduce(out=amax_t[:], in_=tp[:, 0:P], axis=AX.X, op=ALU.max)
         rec = const.tile([P, 1], F32, name="rec")
-        nc.vector.reciprocal(out=rec[:], in_=amax[:])
+        nc.vector.reciprocal(out=rec[:], in_=amax_t[:])
         fac = const.tile([P, 1], F32, name="fac")
         nc.vector.tensor_scalar(out=fac[:], in0=rec[:], scalar1=448.0, scalar2=None, op0=ALU.mult)
 

@@ -131,13 +131,15 @@ def tile_heterogeneousgraphtransformer_pb_kernel(tc, att, scene_reps, Wo, bo, ga
             else:
                 nc.vector.tensor_copy(out=dst32, in_=bank_view)
 
-        def pair_to_codes(raws, name, engs):
+        def pair_to_codes(raws, name, engs, warmers):
             banks = []
             for g in range(NG):
                 banks.append(ps.tile([P, 2, 2, P], F32, tag="bank", name="xt_%s_%d" % (name, g)))
             for tl in range(2):
                 for g in range(NG):
                     turn(banks[g], tl, raws[tl][:].bitcast(F32), g)
+                if warmers:
+                    nc.tensor.matmul(gam_ps[:], lhsT=ones[:], rhs=vecs[:, 1, 0:LO], start=True, stop=True)
             grouped = keep.tile([P, NG * 1024], BF16, name="grp_" + name, align_bytes=64)
             g32 = grouped[:].bitcast(F32).rearrange("p (g t r u) -> p g t r u", g=NG, t=2, u=2)
             for g in range(NG):
@@ -179,7 +181,7 @@ def tile_heterogeneousgraphtransformer_pb_kernel(tc, att, scene_reps, Wo, bo, ga
             if len(grp) == 1:
                 grouped_of[n] = single_to_codes(x_raw[grp[0]], "x%d" % n)
             else:
-                grouped_of[n] = pair_to_codes([x_raw[grp[0]], x_raw[grp[1]]], "x%d" % n, "sss")
+                grouped_of[n] = pair_to_codes([x_raw[grp[0]], x_raw[grp[1]]], "x%d" % n, "sss", False)
 
         def quantise_group(n):
             grp = GROUPS[n]
@@ -276,15 +278,17 @@ def tile_heterogeneousgraphtransformer_pb_kernel(tc, att, scene_reps, Wo, bo, ga
         def store(j):
             nc.sync.dma_start(out=out0_v[j], in_=o_all[:, j, :])
 
-        turn_group(0)
-        quantise_group(0)
-        add_bias(0)
-        for c in range(NC):
-            engs = ""
-            for g in range(NG):
-                engs += "v" if (c * NG + g) in V_WEIGHT_BANKS else "s"
-            grouped = pair_to_codes([w_raw[2 * c], w_raw[2 * c + 1]], "w%d" % c, engs)
-            wq.append(quantise_pair(grouped, "w%d" % c))
+        with tc.manual_schedule(engines={mybir.EngineType.PE}):
+            turn_group(0)
+            nc.tensor.matmul(gam_ps[:], lhsT=ones[:], rhs=vecs[:, 1, 0:LO], start=True, stop=True)
+            quantise_group(0)
+            add_bias(0)
+            for c in range(NC):
+                engs = ""
+                for g in range(NG):
+                    engs += "v" if (c * NG + g) in V_WEIGHT_BANKS else "s"
+                grouped = pair_to_codes([w_raw[2 * c], w_raw[2 * c + 1]], "w%d" % c, engs, True)
+                wq.append(quantise_pair(grouped, "w%d" % c))
         add_bias(1)
         multiply(0)
         turn_group(1)

@@ -28,12 +28,12 @@ EPS = 1e-5
 
 FLOPS = 2 * S * K * D
 
-V_BIAS_TILES = ()
-V_HI_TILES = (7,)
+V_BIAS_TILES = (0, 1)
+V_HI_TILES = (6, 7)
 V_WEIGHT_BANKS = (1, 4, 7)
 LOADS = (("s", 1), ("x", 1), ("x", 2), ("s", 2), ("x", 3), ("x", 4), ("s", 3), ("x", 5), ("x", 6), ("s", 4), ("x", 7), ("s", 5), ("s", 6), ("s", 7))
-GROUPS = ((0,), (1,), (2,), (3, 4), (5, 6), (7,))
-PREFETCH = (3, 4, 5)
+GROUPS = ((0,), (1,), (2,), (3,), (4,), (5,), (6,), (7,))
+PREFETCH = ((3, 4), (5, 6), (7,))
 AMAX = {2: (0, 2), 4: (2, 4), 6: (4, 6), 7: (6, 7), 8: (7, 8)}
 CASTS = (("v", 0, 1536), ("s", 4096, 5120), ("v", 1536, 3072), ("s", 5120, 6144), ("v", 3072, 4096))
 
@@ -131,15 +131,13 @@ def tile_heterogeneousgraphtransformer_pb_kernel(tc, att, scene_reps, Wo, bo, ga
             else:
                 nc.vector.tensor_copy(out=dst32, in_=bank_view)
 
-        def pair_to_codes(raws, name, engs, warmers):
+        def pair_to_codes(raws, name, engs):
             banks = []
             for g in range(NG):
                 banks.append(ps.tile([P, 2, 2, P], F32, tag="bank", name="xt_%s_%d" % (name, g)))
             for tl in range(2):
                 for g in range(NG):
                     turn(banks[g], tl, raws[tl][:].bitcast(F32), g)
-                if warmers:
-                    nc.tensor.matmul(gam_ps[:], lhsT=ones[:], rhs=vecs[:, 1, 0:LO], start=True, stop=True)
             grouped = keep.tile([P, NG * 1024], BF16, name="grp_" + name, align_bytes=64)
             g32 = grouped[:].bitcast(F32).rearrange("p (g t r u) -> p g t r u", g=NG, t=2, u=2)
             for g in range(NG):
@@ -181,7 +179,7 @@ def tile_heterogeneousgraphtransformer_pb_kernel(tc, att, scene_reps, Wo, bo, ga
             if len(grp) == 1:
                 grouped_of[n] = single_to_codes(x_raw[grp[0]], "x%d" % n)
             else:
-                grouped_of[n] = pair_to_codes([x_raw[grp[0]], x_raw[grp[1]]], "x%d" % n, "sss", False)
+                grouped_of[n] = pair_to_codes([x_raw[grp[0]], x_raw[grp[1]]], "x%d" % n, "sss")
 
         def quantise_group(n):
             grp = GROUPS[n]
@@ -278,17 +276,15 @@ def tile_heterogeneousgraphtransformer_pb_kernel(tc, att, scene_reps, Wo, bo, ga
         def store(j):
             nc.sync.dma_start(out=out0_v[j], in_=o_all[:, j, :])
 
-        with tc.manual_schedule(engines={mybir.EngineType.PE}):
-            turn_group(0)
-            nc.tensor.matmul(gam_ps[:], lhsT=ones[:], rhs=vecs[:, 1, 0:LO], start=True, stop=True)
-            quantise_group(0)
-            add_bias(0)
-            for c in range(NC):
-                engs = ""
-                for g in range(NG):
-                    engs += "v" if (c * NG + g) in V_WEIGHT_BANKS else "s"
-                grouped = pair_to_codes([w_raw[2 * c], w_raw[2 * c + 1]], "w%d" % c, engs, True)
-                wq.append(quantise_pair(grouped, "w%d" % c))
+        turn_group(0)
+        quantise_group(0)
+        add_bias(0)
+        for c in range(NC):
+            engs = ""
+            for g in range(NG):
+                engs += "v" if (c * NG + g) in V_WEIGHT_BANKS else "s"
+            grouped = pair_to_codes([w_raw[2 * c], w_raw[2 * c + 1]], "w%d" % c, engs)
+            wq.append(quantise_pair(grouped, "w%d" % c))
         add_bias(1)
         multiply(0)
         turn_group(1)
@@ -303,7 +299,8 @@ def tile_heterogeneousgraphtransformer_pb_kernel(tc, att, scene_reps, Wo, bo, ga
             if i + 2 < NT:
                 multiply(i + 2)
             if i < len(PREFETCH):
-                turn_group(PREFETCH[i])
+                for n in PREFETCH[i]:
+                    turn_group(n)
             if i + 1 < NT:
                 residual_and_stats(i + 1)
             if i < NT:
@@ -317,7 +314,8 @@ def tile_heterogeneousgraphtransformer_pb_kernel(tc, att, scene_reps, Wo, bo, ga
             if i + 3 < NT:
                 add_bias(i + 3)
             if i < len(PREFETCH):
-                quantise_group(PREFETCH[i])
+                for n in PREFETCH[i]:
+                    quantise_group(n)
 
         pmax = const.tile([P, 1], F32, name="pmax")
         nc.vector.tensor_reduce(out=pmax[:], in_=pm[:], axis=AX.X, op=ALU.max)

@@ -34,7 +34,7 @@ V_WEIGHT_BANKS = (1, 4, 7)
 LOADS = (("s", 1), ("x", 1), ("x", 2), ("s", 2), ("x", 3), ("x", 4), ("s", 3), ("x", 5), ("x", 6), ("s", 4), ("x", 7), ("s", 5), ("s", 6), ("s", 7))
 GROUPS = ((0,), (1,), (2,), (3,), (4,), (5,), (6,), (7,))
 PREFETCH = ((3, 4), (5, 6), (7,))
-AMAX = {2: (0, 2), 4: (2, 4), 6: (4, 6), 7: (6, 7), 8: (7, 8)}
+AMAX = {4: (0, 2), 6: (2, 4), 7: (4, 6), 8: (6, 7), 9: (7, 8)}
 CASTS = (("v", 0, 1536), ("s", 4096, 5120), ("v", 1536, 3072), ("s", 5120, 6144), ("v", 3072, 4096))
 
 
@@ -221,7 +221,7 @@ def tile_heterogeneousgraphtransformer_pb_kernel(tc, att, scene_reps, Wo, bo, ga
 
         def residual_and_stats(j):
             acc_lo, acc_hi = accs[j]
-            y = work.tile([P, D], F32, tag="y", name="y", bufs=4)
+            y = work.tile([P, D], F32, tag="y", name="y", bufs=5)
             nc.vector.tensor_tensor(out=y[:, 0:LO], in0=acc_lo[:, 0:LO], in1=srb[j][:, 0:LO], op=ALU.add)
             nc.vector.tensor_tensor(out=y[:, LO:D], in0=acc_hi[:, 0:HI], in1=srb[j][:, LO:D], op=ALU.add)
             col = slice(j, j + 1)
@@ -239,7 +239,7 @@ def tile_heterogeneousgraphtransformer_pb_kernel(tc, att, scene_reps, Wo, bo, ga
         def centre(j):
             y = ys[j]
             col = slice(j, j + 1)
-            t = work.tile([P, D], F32, tag="t", name="t", bufs=3)
+            t = work.tile([P, D], F32, tag="t", name="t", bufs=4)
             ts[j] = t
             nc.vector.scalar_tensor_tensor(
                 out=t[:, 0:LO], in0=y[:, 0:LO], scalar=negmu[:, col], in1=gam_ps[:], op0=ALU.add, op1=ALU.mult
@@ -295,7 +295,7 @@ def tile_heterogeneousgraphtransformer_pb_kernel(tc, att, scene_reps, Wo, bo, ga
         quantise_group(2)
         add_bias(2)
 
-        for i in range(NT + 1):
+        for i in range(NT + 2):
             if i + 2 < NT:
                 multiply(i + 2)
             if i < len(PREFETCH):
@@ -307,10 +307,10 @@ def tile_heterogeneousgraphtransformer_pb_kernel(tc, att, scene_reps, Wo, bo, ga
                 centre(i)
             if i in AMAX:
                 amax(AMAX[i][0], AMAX[i][1])
-            if i >= 1:
-                store(i - 1)
-            if i < NT:
-                scale_shift(i)
+            if i >= 2:
+                store(i - 2)
+            if 1 <= i <= NT:
+                scale_shift(i - 1)
             if i + 3 < NT:
                 add_bias(i + 3)
             if i < len(PREFETCH):

@@ -28,13 +28,9 @@ EPS = 1e-5
 
 FLOPS = 2 * S * K * D
 
-V_BIAS_TILES = (0, 1)
-V_HI_TILES = (6, 7)
+G_HI_TILES = (0, 1, 2, 3, 4, 5)
 V_WEIGHT_BANKS = (1, 4, 7)
 LOADS = (("s", 1), ("x", 1), ("x", 2), ("s", 2), ("x", 3), ("x", 4), ("s", 3), ("x", 5), ("x", 6), ("s", 4), ("x", 7), ("s", 5), ("s", 6), ("s", 7))
-GROUPS = ((0,), (1,), (2,), (3,), (4,), (5,), (6,), (7,))
-PREFETCH = ((3, 4), (5, 6), (7,))
-AMAX = {4: (0, 2), 6: (2, 4), 7: (4, 6), 8: (6, 7), 9: (7, 8)}
 CASTS = (("v", 0, 1536), ("s", 4096, 5120), ("v", 1536, 3072), ("s", 5120, 6144), ("v", 3072, 4096))
 
 
@@ -51,6 +47,7 @@ def tile_heterogeneousgraphtransformer_pb_kernel(tc, att, scene_reps, Wo, bo, ga
         work = ctx.enter_context(tc.tile_pool(name="work", bufs=3))
         ps_gb = ctx.enter_context(tc.psum_pool(name="ps_gb", bufs=1))
         ps = ctx.enter_context(tc.psum_pool(name="ps", bufs=6))
+        ctx.enter_context(tc.manual_schedule())
 
         zero_t = const.tile([P, 1], F32, name="zero_t")
         nc.vector.memset(zero_t[:], 0.0)
@@ -125,87 +122,84 @@ def tile_heterogeneousgraphtransformer_pb_kernel(tc, att, scene_reps, Wo, bo, ga
             for u in range(2):
                 nc.tensor.transpose(dst_bank[:, slot, u, :], words[:, 256 * g + u : 256 * (g + 1) : 2], ident[:])
 
-        def empty(eng, dst32, bank_view):
-            if eng == "s":
-                nc.scalar.copy(out=dst32, in_=bank_view)
-            else:
-                nc.vector.tensor_copy(out=dst32, in_=bank_view)
+        w_banks = {}
+        w_grouped = {}
+        wq = {}
 
-        def pair_to_codes(raws, name, engs):
+        def turn_w(c):
             banks = []
             for g in range(NG):
-                banks.append(ps.tile([P, 2, 2, P], F32, tag="bank", name="xt_%s_%d" % (name, g)))
+                banks.append(ps.tile([P, 2, 2, P], F32, tag="bank", name="wt_%d_%d" % (c, g)))
             for tl in range(2):
                 for g in range(NG):
-                    turn(banks[g], tl, raws[tl][:].bitcast(F32), g)
-            grouped = keep.tile([P, NG * 1024], BF16, name="grp_" + name, align_bytes=64)
+                    turn(banks[g], tl, w_raw[2 * c + tl][:].bitcast(F32), g)
+            w_banks[c] = banks
+
+        def copy_w(c):
+            grouped = keep.tile([P, NG * 1024], BF16, name="grp_w%d" % c, align_bytes=64)
             g32 = grouped[:].bitcast(F32).rearrange("p (g t r u) -> p g t r u", g=NG, t=2, u=2)
             for g in range(NG):
-                empty(engs[g], g32[:, g], banks[g][:].rearrange("p t u r -> p t r u"))
-            return grouped
+                src = w_banks[c][g][:].rearrange("p t u r -> p t r u")
+                if (c * NG + g) in V_WEIGHT_BANKS:
+                    nc.vector.tensor_copy(out=g32[:, g], in_=src)
+                else:
+                    nc.scalar.copy(out=g32[:, g], in_=src)
+            w_grouped[c] = grouped
 
-        def quantise_pair(grouped, name):
-            codes = keep.tile([P, NG * 256], U32, name="c_" + name, align_bytes=64)
-            scales = keep.tile([P, NG * 256], U8, name="s_" + name, align_bytes=64)
+        def quantise_w(c):
+            grouped = w_grouped[c]
+            codes = keep.tile([P, NG * 256], U32, name="c_w%d" % c, align_bytes=64)
+            scales = keep.tile([P, NG * 256], U8, name="s_w%d" % c, align_bytes=64)
             nc.vector.quantize_mx(out=codes[:, 0:512].bitcast(FP8X4), scales=scales[:, 0:512], in_=grouped[:, 0:2048])
             nc.vector.quantize_mx(out=codes[:, 512:768].bitcast(FP8X4), scales=scales[:, 512:768], in_=grouped[:, 2048:3072])
-            return codes, scales
+            wq[c] = (codes, scales)
 
-        def single_to_codes(raw, name):
-            words = raw[:].bitcast(F32)
-            xa = ps.tile([P, 2, 2, P], F32, tag="bank", name="xa_" + name)
-            xb = ps.tile([P, 2, 2, P], F32, tag="bank", name="xb_" + name)
+        x_banks = {}
+        x_grouped = {}
+        xq = {}
+
+        def turn_x(j):
+            words = x_raw[j][:].bitcast(F32)
+            xa = ps.tile([P, 2, 2, P], F32, tag="bank", name="xa_%d" % j)
+            xb = ps.tile([P, 2, 2, P], F32, tag="bank", name="xb_%d" % j)
             turn(xa, 0, words, 0)
             turn(xa, 1, words, 1)
             turn(xb, 0, words, 2)
-            grouped = keep.tile([P, NG * 512], BF16, name="grp_" + name, align_bytes=64)
-            g32 = grouped[:].bitcast(F32).rearrange("p (g r u) -> p g r u", g=NG, u=2)
-            nc.scalar.copy(out=g32[:, 0:2], in_=xa[:].rearrange("p g u r -> p g r u"))
-            nc.scalar.copy(out=g32[:, 2:3], in_=xb[:, 0:1].rearrange("p g u r -> p g r u"))
-            return grouped
+            x_banks[j] = (xa, xb)
 
-        def quantise_single(grouped, name):
-            codes = keep.tile([P, NG * P], U32, name="c_" + name, align_bytes=64)
-            scales = keep.tile([P, NG * P], U8, name="s_" + name, align_bytes=64)
+        def copy_x(j, part):
+            if j not in x_grouped:
+                x_grouped[j] = keep.tile([P, NG * 512], BF16, name="grp_x%d" % j, align_bytes=64)
+            g32 = x_grouped[j][:].bitcast(F32).rearrange("p (g r u) -> p g r u", g=NG, u=2)
+            if part == 0:
+                nc.scalar.copy(out=g32[:, 0:2], in_=x_banks[j][0][:].rearrange("p g u r -> p g r u"))
+            else:
+                nc.scalar.copy(out=g32[:, 2:3], in_=x_banks[j][1][:, 0:1].rearrange("p g u r -> p g r u"))
+
+        def quantise_x(j):
+            grouped = x_grouped[j]
+            codes = keep.tile([P, NG * P], U32, name="c_x%d" % j, align_bytes=64)
+            scales = keep.tile([P, NG * P], U8, name="s_x%d" % j, align_bytes=64)
             nc.vector.quantize_mx(out=codes[:, 0:256].bitcast(FP8X4), scales=scales[:, 0:256], in_=grouped[:, 0:1024])
             nc.vector.quantize_mx(out=codes[:, 256:384].bitcast(FP8X4), scales=scales[:, 256:384], in_=grouped[:, 1024:1536])
-            return codes, scales
-
-        grouped_of = {}
-        tok = {}
-
-        def turn_group(n):
-            grp = GROUPS[n]
-            if len(grp) == 1:
-                grouped_of[n] = single_to_codes(x_raw[grp[0]], "x%d" % n)
-            else:
-                grouped_of[n] = pair_to_codes([x_raw[grp[0]], x_raw[grp[1]]], "x%d" % n, "sss")
-
-        def quantise_group(n):
-            grp = GROUPS[n]
-            if len(grp) == 1:
-                codes, scales = quantise_single(grouped_of[n], "x%d" % n)
-                tok[grp[0]] = (codes, scales, 0, P)
-            else:
-                codes, scales = quantise_pair(grouped_of[n], "x%d" % n)
-                tok[grp[0]] = (codes, scales, 0, 2 * P)
-                tok[grp[1]] = (codes, scales, P, 2 * P)
+            xq[j] = (codes, scales)
 
         def add_bias(j):
-            eng = nc.vector if j in V_BIAS_TILES else nc.gpsimd
-            eng.tensor_tensor(out=srb[j][:], in0=sr[j][:], in1=bo_sb[:], op=ALU.add)
+            nc.gpsimd.tensor_tensor(out=srb[j][:], in0=sr[j][:], in1=bo_sb[:], op=ALU.add)
 
-        wq = []
         accs = {}
 
-        def multiply(j):
-            codes, scales, first, step = tok[j]
-            acc_lo = ps.tile([P, 512], F32, tag="bank", name="acc_lo")
-            acc_hi = ps.tile([P, 512], F32, tag="bank", name="acc_hi")
+        def multiply(j, chunks):
+            codes, scales = xq[j]
+            if j not in accs:
+                acc_lo = ps.tile([P, 512], F32, tag="bank", name="acc_lo")
+                acc_hi = ps.tile([P, 512], F32, tag="bank", name="acc_hi")
+                accs[j] = (acc_lo, acc_hi)
+            acc_lo, acc_hi = accs[j]
             outs = (acc_lo[:, 0:CW], acc_lo[:, CW : 2 * CW], acc_hi[:, 0:CW])
-            for c in range(NC):
+            for c in chunks:
                 for g in range(NG):
-                    cols = slice(first + g * step, first + g * step + P)
+                    cols = slice(g * P, (g + 1) * P)
                     nc.tensor.matmul_mx(
                         out=outs[c],
                         lhsT=codes[:, cols].bitcast(FP8X4),
@@ -215,24 +209,29 @@ def tile_heterogeneousgraphtransformer_pb_kernel(tc, att, scene_reps, Wo, bo, ga
                         start=(g == 0),
                         stop=(g == NG - 1),
                     )
-            accs[j] = (acc_lo, acc_hi)
 
         ys = {}
 
-        def residual_and_stats(j):
+        def residual(j):
             acc_lo, acc_hi = accs[j]
             y = work.tile([P, D], F32, tag="y", name="y", bufs=5)
             nc.vector.tensor_tensor(out=y[:, 0:LO], in0=acc_lo[:, 0:LO], in1=srb[j][:, 0:LO], op=ALU.add)
             nc.vector.tensor_tensor(out=y[:, LO:D], in0=acc_hi[:, 0:HI], in1=srb[j][:, LO:D], op=ALU.add)
-            col = slice(j, j + 1)
-            junk = work.tile([P, D], BF16, tag="junk", name="junk", bufs=2)
-            nc.scalar.activation(out=junk[:], in_=y[:], func=ACT.Identity, scale=-1.0 / D, accum_out=negmu[:, col])
-            junk2 = work.tile([P, D], BF16, tag="junk", name="junk2", bufs=2)
-            nc.scalar.activation(out=junk2[:], in_=y[:], func=ACT.Square, bias=negmu[:, col], accum_out=ssq[:, col])
-            nc.scalar.activation(
-                out=rstd[:, col], in_=ssq[:, col], func=ACT.Abs_reciprocal_sqrt, bias=eps_t[:, 0:1], scale=1.0 / D
-            )
             ys[j] = y
+
+        def stats(j, part):
+            y = ys[j]
+            col = slice(j, j + 1)
+            if part == 0:
+                junk = work.tile([P, D], BF16, tag="junk", name="junk", bufs=2)
+                nc.scalar.activation(out=junk[:], in_=y[:], func=ACT.Identity, scale=-1.0 / D, accum_out=negmu[:, col])
+            elif part == 1:
+                junk2 = work.tile([P, D], BF16, tag="junk", name="junk2", bufs=2)
+                nc.scalar.activation(out=junk2[:], in_=y[:], func=ACT.Square, bias=negmu[:, col], accum_out=ssq[:, col])
+            else:
+                nc.scalar.activation(
+                    out=rstd[:, col], in_=ssq[:, col], func=ACT.Abs_reciprocal_sqrt, bias=eps_t[:, 0:1], scale=1.0 / D
+                )
 
         ts = {}
 
@@ -244,29 +243,31 @@ def tile_heterogeneousgraphtransformer_pb_kernel(tc, att, scene_reps, Wo, bo, ga
             nc.vector.scalar_tensor_tensor(
                 out=t[:, 0:LO], in0=y[:, 0:LO], scalar=negmu[:, col], in1=gam_ps[:], op0=ALU.add, op1=ALU.mult
             )
-            if j in V_HI_TILES:
+            if j not in G_HI_TILES:
                 nc.vector.scalar_tensor_tensor(
                     out=t[:, LO:D], in0=y[:, LO:D], scalar=negmu[:, col], in1=g_hi[:], op0=ALU.add, op1=ALU.mult
                 )
 
         def scale_shift(j):
-            y = ys[j]
             t = ts[j]
             col = slice(j, j + 1)
             nc.vector.scalar_tensor_tensor(
                 out=o_all[:, j, 0:LO], in0=t[:, 0:LO], scalar=rstd[:, col], in1=bet_ps[:], op0=ALU.mult, op1=ALU.add
             )
-            if j in V_HI_TILES:
+            if j not in G_HI_TILES:
                 nc.vector.scalar_tensor_tensor(
                     out=o_all[:, j, LO:D], in0=t[:, LO:D], scalar=rstd[:, col], in1=b_hi[:], op0=ALU.mult, op1=ALU.add
                 )
-            else:
-                z = work.tile([P, HI], F32, tag="z", name="z", bufs=3)
-                nc.gpsimd.tensor_scalar(
-                    out=z[:], in0=y[:, LO:D], scalar1=negmu[:, col], scalar2=rstd[:, col], op0=ALU.add, op1=ALU.mult
-                )
-                nc.gpsimd.tensor_tensor(out=z[:], in0=z[:], in1=g_hi[:], op=ALU.mult)
-                nc.gpsimd.tensor_tensor(out=o_all[:, j, LO:D], in0=z[:], in1=b_hi[:], op=ALU.add)
+
+        def hi_on_gpsimd(j):
+            y = ys[j]
+            col = slice(j, j + 1)
+            z = work.tile([P, HI], F32, tag="z", name="z", bufs=3)
+            nc.gpsimd.tensor_scalar(
+                out=z[:], in0=y[:, LO:D], scalar1=negmu[:, col], scalar2=rstd[:, col], op0=ALU.add, op1=ALU.mult
+            )
+            nc.gpsimd.tensor_tensor(out=z[:], in0=z[:], in1=g_hi[:], op=ALU.mult)
+            nc.gpsimd.tensor_tensor(out=o_all[:, j, LO:D], in0=z[:], in1=b_hi[:], op=ALU.add)
 
         def amax(j0, j1):
             nc.vector.tensor_reduce(
@@ -276,46 +277,63 @@ def tile_heterogeneousgraphtransformer_pb_kernel(tc, att, scene_reps, Wo, bo, ga
         def store(j):
             nc.sync.dma_start(out=out0_v[j], in_=o_all[:, j, :])
 
-        turn_group(0)
-        quantise_group(0)
+        turn_x(0)
+        copy_x(0, 0)
+        copy_x(0, 1)
+        quantise_x(0)
         add_bias(0)
         for c in range(NC):
-            engs = ""
-            for g in range(NG):
-                engs += "v" if (c * NG + g) in V_WEIGHT_BANKS else "s"
-            grouped = pair_to_codes([w_raw[2 * c], w_raw[2 * c + 1]], "w%d" % c, engs)
-            wq.append(quantise_pair(grouped, "w%d" % c))
+            turn_w(c)
+            copy_w(c)
+            quantise_w(c)
         add_bias(1)
-        multiply(0)
-        turn_group(1)
-        quantise_group(1)
-        residual_and_stats(0)
-        multiply(1)
-        turn_group(2)
-        quantise_group(2)
-        add_bias(2)
+        multiply(0, (0, 1))
+        turn_x(1)
+        copy_x(1, 0)
+        copy_x(1, 1)
+        multiply(0, (2,))
+        quantise_x(1)
+        for j in range(2, 3):
+            turn_x(j)
+            copy_x(j, 0)
+            copy_x(j, 1)
+        for j in range(2, 2):
+            quantise_x(j)
+        for j in range(2, 5):
+            add_bias(j)
 
-        for i in range(NT + 2):
-            if i + 2 < NT:
-                multiply(i + 2)
-            if i < len(PREFETCH):
-                for n in PREFETCH[i]:
-                    turn_group(n)
-            if i + 1 < NT:
-                residual_and_stats(i + 1)
-            if i < NT:
-                centre(i)
-            if i in AMAX:
-                amax(AMAX[i][0], AMAX[i][1])
-            if i >= 2:
-                store(i - 2)
-            if 1 <= i <= NT:
-                scale_shift(i - 1)
-            if i + 3 < NT:
-                add_bias(i + 3)
-            if i < len(PREFETCH):
-                for n in PREFETCH[i]:
-                    quantise_group(n)
+        for j in range(NT + 4):
+            if j + 3 < NT:
+                turn_x(j + 3)
+            if j + 1 < NT:
+                multiply(j + 1, (0, 1, 2))
+            if j < NT:
+                residual(j)
+                stats(j, 0)
+            if j + 3 < NT:
+                copy_x(j + 3, 0)
+            if j < NT:
+                stats(j, 1)
+            if j + 3 < NT:
+                copy_x(j + 3, 1)
+            if j < NT:
+                stats(j, 2)
+            if 0 <= j - 1 < NT:
+                centre(j - 1)
+            if 0 <= j - 2 < NT:
+                scale_shift(j - 2)
+            if j - 1 in G_HI_TILES:
+                hi_on_gpsimd(j - 1)
+            if 5 <= j + 4 < NT:
+                add_bias(j + 4)
+            if 0 <= j - 4 < NT - 1:
+                amax(j - 4, j - 4 + 1)
+            if 0 <= j - 3 < NT:
+                store(j - 3)
+            if j + 2 < NT:
+                quantise_x(j + 2)
+        amax(NT - 1, NT)
+
 
         pmax = const.tile([P, 1], F32, name="pmax")
         nc.vector.tensor_reduce(out=pmax[:], in_=pm[:], axis=AX.X, op=ALU.max)

@@ -56,10 +56,14 @@ def tile_heterogeneousgraphtransformer_pb_kernel(tc, att, scene_reps, Wo, bo, ga
         warm = const.tile([P, 1], F32, name="warm")
         nc.scalar.activation(out=warm[:], in_=eps_t[:], func=ACT.Abs_reciprocal_sqrt)
 
-        vecs = const.tile([P, 3, D], BF16, name="vecs")
-        nc.vector.memset(vecs[:].rearrange("p v d -> p (v d)").bitcast(F32), 0.0)
-        for i, v in enumerate((bo, gamma, beta)):
-            nc.scalar.dma_start(out=vecs[0:1, i, :], in_=v.rearrange("(o d) -> o d", o=1))
+        vec_rows = []
+        for i in range(3):
+            vec_rows.append(const.tile([P, D], BF16, name="vec_row%d" % i))
+            nc.gpsimd.memset(vec_rows[i][:].bitcast(F32), 0.0)
+
+        def load_vec(i):
+            nc.sync.dma_start(out=vec_rows[i][0:1, :], in_=(bo, gamma, beta)[i].rearrange("(o d) -> o d", o=1))
+
         ones = const.tile([P, P], BF16, name="ones")
         nc.vector.memset(ones[:], 1.0)
         ident = const.tile([P, P], F32, name="ident")
@@ -80,10 +84,17 @@ def tile_heterogeneousgraphtransformer_pb_kernel(tc, att, scene_reps, Wo, bo, ga
         def load_sr(j):
             nc.sync.dma_start(out=sr[j][:], in_=sr_v[j])
 
+        load_vec(0)
         load_x(0)
+        load_vec(1)
+        load_vec(2)
         load_sr(0)
-        for r in range(2 * NC):
-            nc.sync.dma_start(out=w_raw[r][:], in_=Wo[r * P : (r + 1) * P, :])
+        nc.sync.dma_start(out=w_raw[0][:], in_=Wo[0 * P : 1 * P, :])
+        nc.sync.dma_start(out=w_raw[1][:], in_=Wo[1 * P : 2 * P, :])
+        nc.sync.dma_start(out=w_raw[2][:], in_=Wo[2 * P : 3 * P, :])
+        nc.sync.dma_start(out=w_raw[3][:], in_=Wo[3 * P : 4 * P, :])
+        nc.sync.dma_start(out=w_raw[4][:], in_=Wo[4 * P : 5 * P, :])
+        nc.sync.dma_start(out=w_raw[5][:], in_=Wo[5 * P : 6 * P, :])
         for what, j in LOADS:
             if what == "x":
                 load_x(j)
@@ -95,24 +106,29 @@ def tile_heterogeneousgraphtransformer_pb_kernel(tc, att, scene_reps, Wo, bo, ga
         bo_sb = const.tile([P, D], BF16, name="bo_sb")
         g_hi = const.tile([P, HI], F32, name="g_hi")
         b_hi = const.tile([P, HI], F32, name="b_hi")
-        bc1 = ps.tile([P, 512], F32, tag="bank", name="bc1")
-        bc2 = ps.tile([P, 512], F32, tag="bank", name="bc2")
-        bc3 = ps.tile([P, 512], F32, tag="bank", name="bc3")
-        nc.tensor.matmul(bc1[:], lhsT=ones[:], rhs=vecs[:, 0, 0:LO], start=True, stop=True)
-        nc.tensor.matmul(bc2[:, 0:HI], lhsT=ones[:], rhs=vecs[:, 0, LO:D], start=True, stop=True)
-        nc.tensor.matmul(bc2[:, HI : 2 * HI], lhsT=ones[:], rhs=vecs[:, 1, LO:D], start=True, stop=True)
-        nc.tensor.matmul(bc3[:, 0:HI], lhsT=ones[:], rhs=vecs[:, 2, LO:D], start=True, stop=True)
-        nc.tensor.matmul(gam_ps[:], lhsT=ones[:], rhs=vecs[:, 1, 0:LO], start=True, stop=True)
-        nc.tensor.matmul(bet_ps[:], lhsT=ones[:], rhs=vecs[:, 2, 0:LO], start=True, stop=True)
-        nc.scalar.copy(out=bo_sb[:, 0:LO], in_=bc1[:])
-        nc.scalar.copy(out=bo_sb[:, LO:D], in_=bc2[:, 0:HI])
-        nc.scalar.copy(out=g_hi[:], in_=bc2[:, HI : 2 * HI])
-        nc.scalar.copy(out=b_hi[:], in_=bc3[:, 0:HI])
+
+        def spread_bo():
+            bc1 = ps.tile([P, 512], F32, tag="bank", name="bc1")
+            bc2 = ps.tile([P, 512], F32, tag="bank", name="bc2")
+            nc.tensor.matmul(bc1[:], lhsT=ones[:], rhs=vec_rows[0][:, 0:LO], start=True, stop=True)
+            nc.tensor.matmul(bc2[:, 0:HI], lhsT=ones[:], rhs=vec_rows[0][:, LO:D], start=True, stop=True)
+            nc.scalar.copy(out=bo_sb[:, 0:LO], in_=bc1[:])
+            nc.scalar.copy(out=bo_sb[:, LO:D], in_=bc2[:, 0:HI])
+
+        def spread_gamma_beta():
+            bc3 = ps.tile([P, 512], F32, tag="bank", name="bc3")
+            nc.tensor.matmul(bc3[:, 0:HI], lhsT=ones[:], rhs=vec_rows[1][:, LO:D], start=True, stop=True)
+            nc.tensor.matmul(bc3[:, HI : 2 * HI], lhsT=ones[:], rhs=vec_rows[2][:, LO:D], start=True, stop=True)
+            nc.tensor.matmul(gam_ps[:], lhsT=ones[:], rhs=vec_rows[1][:, 0:LO], start=True, stop=True)
+            nc.tensor.matmul(bet_ps[:], lhsT=ones[:], rhs=vec_rows[2][:, 0:LO], start=True, stop=True)
+            nc.scalar.copy(out=g_hi[:], in_=bc3[:, 0:HI])
+            nc.scalar.copy(out=b_hi[:], in_=bc3[:, HI : 2 * HI])
 
         srb = []
         for j in range(NT):
             srb.append(keep.tile([P, D], F32, name="srb%d" % j))
-        o_all = keep.tile([P, NT, D], F32, name="o_all")
+        o_ext = keep.tile([P, NT * D + 1], F32, name="o_ext")
+        o_all = o_ext[:, 0 : NT * D].rearrange("p (j d) -> p j d", j=NT)
         negmu = const.tile([P, NT], F32, name="negmu")
         ssq = const.tile([P, NT], F32, name="ssq")
         rstd = const.tile([P, NT], F32, name="rstd")
@@ -212,12 +228,15 @@ def tile_heterogeneousgraphtransformer_pb_kernel(tc, att, scene_reps, Wo, bo, ga
 
         ys = {}
 
-        def residual(j):
+        def residual(j, parts=(0, 1)):
             acc_lo, acc_hi = accs[j]
-            y = work.tile([P, D], F32, tag="y", name="y", bufs=5)
-            nc.vector.tensor_tensor(out=y[:, 0:LO], in0=acc_lo[:, 0:LO], in1=srb[j][:, 0:LO], op=ALU.add)
-            nc.vector.tensor_tensor(out=y[:, LO:D], in0=acc_hi[:, 0:HI], in1=srb[j][:, LO:D], op=ALU.add)
-            ys[j] = y
+            if j not in ys:
+                ys[j] = work.tile([P, D], F32, tag="y", name="y", bufs=5)
+            y = ys[j]
+            if 0 in parts:
+                nc.vector.tensor_tensor(out=y[:, 0:LO], in0=acc_lo[:, 0:LO], in1=srb[j][:, 0:LO], op=ALU.add)
+            if 1 in parts:
+                nc.vector.tensor_tensor(out=y[:, LO:D], in0=acc_hi[:, 0:HI], in1=srb[j][:, LO:D], op=ALU.add)
 
         def stats(j, part):
             y = ys[j]
@@ -259,48 +278,72 @@ def tile_heterogeneousgraphtransformer_pb_kernel(tc, att, scene_reps, Wo, bo, ga
                     out=o_all[:, j, LO:D], in0=t[:, LO:D], scalar=rstd[:, col], in1=b_hi[:], op0=ALU.mult, op1=ALU.add
                 )
 
-        def hi_on_gpsimd(j):
+        zs = {}
+
+        def hi_on_gpsimd(j, parts=(0, 1, 2)):
             y = ys[j]
             col = slice(j, j + 1)
-            z = work.tile([P, HI], F32, tag="z", name="z", bufs=3)
-            nc.gpsimd.tensor_scalar(
+            if j not in zs:
+                zs[j] = work.tile([P, HI], F32, tag="z", name="z", bufs=3)
+            z = zs[j]
+            if 0 in parts:
+              nc.gpsimd.tensor_scalar(
                 out=z[:], in0=y[:, LO:D], scalar1=negmu[:, col], scalar2=rstd[:, col], op0=ALU.add, op1=ALU.mult
             )
-            nc.gpsimd.tensor_tensor(out=z[:], in0=z[:], in1=g_hi[:], op=ALU.mult)
-            nc.gpsimd.tensor_tensor(out=o_all[:, j, LO:D], in0=z[:], in1=b_hi[:], op=ALU.add)
+            if 1 in parts:
+                nc.gpsimd.tensor_tensor(out=z[:], in0=z[:], in1=g_hi[:], op=ALU.mult)
+            if 2 in parts:
+                nc.gpsimd.tensor_tensor(out=o_all[:, j, LO:D], in0=z[:], in1=b_hi[:], op=ALU.add)
 
         def amax(j0, j1):
             nc.vector.tensor_reduce(
                 out=pm[:, j0:j1], in_=o_all[:, j0:j1, :], axis=AX.X, op=ALU.max, apply_absolute_value=True
             )
 
+        pmax = const.tile([P, 1], F32, name="pmax")
+
+        def amax_before_last():
+            nc.vector.tensor_reduce(out=o_ext[:, NT * D : NT * D + 1], in_=pm[:, 0 : NT - 2], axis=AX.X, op=ALU.max)
+
+        def amax_last():
+            nc.vector.tensor_reduce(
+                out=pmax[:], in_=o_ext[:, (NT - 2) * D : NT * D + 1], axis=AX.X, op=ALU.max, apply_absolute_value=True
+            )
+
         def store(j):
             nc.sync.dma_start(out=out0_v[j], in_=o_all[:, j, :])
 
+        spread_bo()
+        spread_gamma_beta()
         turn_x(0)
         copy_x(0, 0)
         copy_x(0, 1)
         quantise_x(0)
         add_bias(0)
-        for c in range(NC):
-            turn_w(c)
-            copy_w(c)
-            quantise_w(c)
+        turn_w(0)
+        copy_w(0)
+        quantise_w(0)
+        turn_w(1)
+        copy_w(1)
+        quantise_w(1)
+        turn_w(2)
+        copy_w(2)
+        quantise_w(2)
         add_bias(1)
         multiply(0, (0, 1))
         turn_x(1)
         copy_x(1, 0)
         copy_x(1, 1)
         multiply(0, (2,))
+        residual(0, (0,))
         quantise_x(1)
-        for j in range(2, 3):
-            turn_x(j)
-            copy_x(j, 0)
-            copy_x(j, 1)
-        for j in range(2, 2):
-            quantise_x(j)
-        for j in range(2, 5):
-            add_bias(j)
+        residual(0, (1,))
+        turn_x(2)
+        copy_x(2, 0)
+        copy_x(2, 1)
+        add_bias(2)
+        add_bias(3)
+        add_bias(4)
 
         for j in range(NT + 4):
             if j + 3 < NT:
@@ -308,7 +351,8 @@ def tile_heterogeneousgraphtransformer_pb_kernel(tc, att, scene_reps, Wo, bo, ga
             if j + 1 < NT:
                 multiply(j + 1, (0, 1, 2))
             if j < NT:
-                residual(j)
+                if j > 0:
+                    residual(j)
                 stats(j, 0)
             if j + 3 < NT:
                 copy_x(j + 3, 0)
@@ -320,33 +364,35 @@ def tile_heterogeneousgraphtransformer_pb_kernel(tc, att, scene_reps, Wo, bo, ga
                 stats(j, 2)
             if 0 <= j - 1 < NT:
                 centre(j - 1)
+            if 0 <= j - 4 < NT - 2:
+                amax(j - 4, j - 4 + 1)
             if 0 <= j - 2 < NT:
                 scale_shift(j - 2)
             if j - 1 in G_HI_TILES:
-                hi_on_gpsimd(j - 1)
+                hi_on_gpsimd(j - 1, (0,))
+            if j - 1 - 1 in G_HI_TILES:
+                hi_on_gpsimd(j - 1 - 1, (2,))
             if 5 <= j + 4 < NT:
                 add_bias(j + 4)
-            if 0 <= j - 4 < NT - 1:
-                amax(j - 4, j - 4 + 1)
+            if j - 1 in G_HI_TILES:
+                hi_on_gpsimd(j - 1, (1,))
             if 0 <= j - 3 < NT:
                 store(j - 3)
             if j + 2 < NT:
                 quantise_x(j + 2)
-        amax(NT - 1, NT)
+        amax_before_last()
+        amax_last()
 
 
-        pmax = const.tile([P, 1], F32, name="pmax")
-        nc.vector.tensor_reduce(out=pmax[:], in_=pm[:], axis=AX.X, op=ALU.max)
         tp = ps.tile([P, 512], F32, tag="bank", name="tp")
         nc.tensor.transpose(tp[:, 0:P], pmax[:, 0:1].to_broadcast([P, P]), ident[:])
-        amax_t = const.tile([P, 1], F32, name="amax_t")
-        nc.vector.tensor_reduce(out=amax_t[:], in_=tp[:, 0:P], axis=AX.X, op=ALU.max)
-        rec = const.tile([P, 1], F32, name="rec")
-        nc.vector.reciprocal(out=rec[:], in_=amax_t[:])
+        scaled = const.tile([P, P], F32, name="scaled")
+        s_t = const.tile([P, 1], F32, name="s_t")
+        nc.vector.tensor_scalar(out=scaled[:], in0=tp[:, 0:P], scalar1=1.0 / 448.0, scalar2=None, op0=ALU.mult, op1=ALU.max, accum_out=s_t[:])
         fac = const.tile([P, 1], F32, name="fac")
-        nc.vector.tensor_scalar(out=fac[:], in0=rec[:], scalar1=448.0, scalar2=None, op0=ALU.mult)
+        nc.vector.reciprocal(out=fac[:], in_=s_t[:])
 
-        o_flat = o_all[:].rearrange("p j d -> p (j d)")
+        o_flat = o_ext[:, 0 : NT * D]
         for i, (eng, c0, c1) in enumerate(CASTS):
             q = keep.tile([P, c1 - c0], FP8, name="q%d" % i)
             if eng == "v":

@@ -28,8 +28,10 @@ EPS = 1e-5
 
 FLOPS = 2 * S * K * D
 
-G_HI_TILES = (0, 1, 2, 3, 4, 5)
+HIW = 320
+CS = D - HIW
 V_WEIGHT_BANKS = (1, 4, 7)
+V_COPY_TILES = (3, 4, 5,)
 LOADS = (("s", 1), ("x", 1), ("x", 2), ("s", 2), ("x", 3), ("x", 4), ("s", 3), ("x", 5), ("x", 6), ("s", 4), ("x", 7), ("s", 5), ("s", 6), ("s", 7))
 CASTS = (("v", 0, 1536), ("s", 4096, 5120), ("v", 1536, 3072), ("s", 5120, 6144), ("v", 3072, 4096))
 
@@ -104,8 +106,8 @@ def tile_heterogeneousgraphtransformer_pb_kernel(tc, att, scene_reps, Wo, bo, ga
         gam_ps = ps_gb.tile([P, LO], F32, name="gam_ps")
         bet_ps = ps_gb.tile([P, LO], F32, name="bet_ps")
         bo_sb = const.tile([P, D], BF16, name="bo_sb")
-        g_hi = const.tile([P, HI], F32, name="g_hi")
-        b_hi = const.tile([P, HI], F32, name="b_hi")
+        g_hi = const.tile([P, HIW], F32, name="g_hi")
+        b_hi = const.tile([P, HIW], F32, name="b_hi")
 
         def spread_bo():
             bc1 = ps.tile([P, 512], F32, tag="bank", name="bc1")
@@ -117,22 +119,24 @@ def tile_heterogeneousgraphtransformer_pb_kernel(tc, att, scene_reps, Wo, bo, ga
 
         def spread_gamma_beta():
             bc3 = ps.tile([P, 512], F32, tag="bank", name="bc3")
-            nc.tensor.matmul(bc3[:, 0:HI], lhsT=ones[:], rhs=vec_rows[1][:, LO:D], start=True, stop=True)
-            nc.tensor.matmul(bc3[:, HI : 2 * HI], lhsT=ones[:], rhs=vec_rows[2][:, LO:D], start=True, stop=True)
+            bc4 = ps.tile([P, 512], F32, tag="bank", name="bc4")
+            nc.tensor.matmul(bc3[:, 0:HIW], lhsT=ones[:], rhs=vec_rows[1][:, CS:D], start=True, stop=True)
+            nc.tensor.matmul(bc4[:, 0:HIW], lhsT=ones[:], rhs=vec_rows[2][:, CS:D], start=True, stop=True)
             nc.tensor.matmul(gam_ps[:], lhsT=ones[:], rhs=vec_rows[1][:, 0:LO], start=True, stop=True)
             nc.tensor.matmul(bet_ps[:], lhsT=ones[:], rhs=vec_rows[2][:, 0:LO], start=True, stop=True)
-            nc.scalar.copy(out=g_hi[:], in_=bc3[:, 0:HI])
-            nc.scalar.copy(out=b_hi[:], in_=bc3[:, HI : 2 * HI])
+            nc.scalar.copy(out=g_hi[:], in_=bc3[:, 0:HIW])
+            nc.scalar.copy(out=b_hi[:], in_=bc4[:, 0:HIW])
 
         srb = []
         for j in range(NT):
             srb.append(keep.tile([P, D], F32, name="srb%d" % j))
-        o_ext = keep.tile([P, NT * D + 1], F32, name="o_ext")
+        o_ext = keep.tile([P, NT * D + 2], F32, name="o_ext")
         o_all = o_ext[:, 0 : NT * D].rearrange("p (j d) -> p j d", j=NT)
         negmu = const.tile([P, NT], F32, name="negmu")
         ssq = const.tile([P, NT], F32, name="ssq")
         rstd = const.tile([P, NT], F32, name="rstd")
         pm = const.tile([P, NT], F32, name="pm")
+        nmr = const.tile([P, NT], F32, name="nmr")
 
         def turn(dst_bank, slot, words, g):
             for u in range(2):
@@ -189,6 +193,8 @@ def tile_heterogeneousgraphtransformer_pb_kernel(tc, att, scene_reps, Wo, bo, ga
             g32 = x_grouped[j][:].bitcast(F32).rearrange("p (g r u) -> p g r u", g=NG, u=2)
             if part == 0:
                 nc.scalar.copy(out=g32[:, 0:2], in_=x_banks[j][0][:].rearrange("p g u r -> p g r u"))
+            elif j in V_COPY_TILES:
+                nc.vector.tensor_copy(out=g32[:, 2:3], in_=x_banks[j][1][:, 0:1].rearrange("p g u r -> p g r u"))
             else:
                 nc.scalar.copy(out=g32[:, 2:3], in_=x_banks[j][1][:, 0:1].rearrange("p g u r -> p g r u"))
 
@@ -244,13 +250,15 @@ def tile_heterogeneousgraphtransformer_pb_kernel(tc, att, scene_reps, Wo, bo, ga
             if part == 0:
                 junk = work.tile([P, D], BF16, tag="junk", name="junk", bufs=2)
                 nc.scalar.activation(out=junk[:], in_=y[:], func=ACT.Identity, scale=-1.0 / D, accum_out=negmu[:, col])
-            elif part == 1:
+            if part == 1:
                 junk2 = work.tile([P, D], BF16, tag="junk", name="junk2", bufs=2)
                 nc.scalar.activation(out=junk2[:], in_=y[:], func=ACT.Square, bias=negmu[:, col], accum_out=ssq[:, col])
-            else:
+            if part == 2:
                 nc.scalar.activation(
                     out=rstd[:, col], in_=ssq[:, col], func=ACT.Abs_reciprocal_sqrt, bias=eps_t[:, 0:1], scale=1.0 / D
                 )
+            if part == 3:
+                nc.scalar.activation(out=nmr[:, col], in_=negmu[:, col], func=ACT.Copy, scale=rstd[:, col])
 
         ts = {}
 
@@ -260,23 +268,15 @@ def tile_heterogeneousgraphtransformer_pb_kernel(tc, att, scene_reps, Wo, bo, ga
             t = work.tile([P, D], F32, tag="t", name="t", bufs=4)
             ts[j] = t
             nc.vector.scalar_tensor_tensor(
-                out=t[:, 0:LO], in0=y[:, 0:LO], scalar=negmu[:, col], in1=gam_ps[:], op0=ALU.add, op1=ALU.mult
+                out=t[:, 0:CS], in0=y[:, 0:CS], scalar=negmu[:, col], in1=gam_ps[:, 0:CS], op0=ALU.add, op1=ALU.mult
             )
-            if j not in G_HI_TILES:
-                nc.vector.scalar_tensor_tensor(
-                    out=t[:, LO:D], in0=y[:, LO:D], scalar=negmu[:, col], in1=g_hi[:], op0=ALU.add, op1=ALU.mult
-                )
 
         def scale_shift(j):
             t = ts[j]
             col = slice(j, j + 1)
             nc.vector.scalar_tensor_tensor(
-                out=o_all[:, j, 0:LO], in0=t[:, 0:LO], scalar=rstd[:, col], in1=bet_ps[:], op0=ALU.mult, op1=ALU.add
+                out=o_all[:, j, 0:CS], in0=t[:, 0:CS], scalar=rstd[:, col], in1=bet_ps[:, 0:CS], op0=ALU.mult, op1=ALU.add
             )
-            if j not in G_HI_TILES:
-                nc.vector.scalar_tensor_tensor(
-                    out=o_all[:, j, LO:D], in0=t[:, LO:D], scalar=rstd[:, col], in1=b_hi[:], op0=ALU.mult, op1=ALU.add
-                )
 
         zs = {}
 
@@ -284,16 +284,14 @@ def tile_heterogeneousgraphtransformer_pb_kernel(tc, att, scene_reps, Wo, bo, ga
             y = ys[j]
             col = slice(j, j + 1)
             if j not in zs:
-                zs[j] = work.tile([P, HI], F32, tag="z", name="z", bufs=3)
+                zs[j] = work.tile([P, HIW], F32, tag="z", name="z", bufs=3)
             z = zs[j]
             if 0 in parts:
-              nc.gpsimd.tensor_scalar(
-                out=z[:], in0=y[:, LO:D], scalar1=negmu[:, col], scalar2=rstd[:, col], op0=ALU.add, op1=ALU.mult
-            )
+                nc.scalar.activation(out=z[:], in_=y[:, CS:D], func=ACT.Identity, scale=rstd[:, col], bias=nmr[:, col])
             if 1 in parts:
                 nc.gpsimd.tensor_tensor(out=z[:], in0=z[:], in1=g_hi[:], op=ALU.mult)
             if 2 in parts:
-                nc.gpsimd.tensor_tensor(out=o_all[:, j, LO:D], in0=z[:], in1=b_hi[:], op=ALU.add)
+                nc.gpsimd.tensor_tensor(out=o_all[:, j, CS:D], in0=z[:], in1=b_hi[:], op=ALU.add)
 
         def amax(j0, j1):
             nc.vector.tensor_reduce(
@@ -305,9 +303,18 @@ def tile_heterogeneousgraphtransformer_pb_kernel(tc, att, scene_reps, Wo, bo, ga
         def amax_before_last():
             nc.vector.tensor_reduce(out=o_ext[:, NT * D : NT * D + 1], in_=pm[:, 0 : NT - 2], axis=AX.X, op=ALU.max)
 
+        def amax_most_of_last_two():
+            nc.vector.tensor_reduce(
+                out=o_ext[:, NT * D + 1 : NT * D + 2],
+                in_=o_ext[:, (NT - 2) * D : (NT - 1) * D + CS],
+                axis=AX.X,
+                op=ALU.max,
+                apply_absolute_value=True,
+            )
+
         def amax_last():
             nc.vector.tensor_reduce(
-                out=pmax[:], in_=o_ext[:, (NT - 2) * D : NT * D + 1], axis=AX.X, op=ALU.max, apply_absolute_value=True
+                out=pmax[:], in_=o_ext[:, (NT - 1) * D + CS : NT * D + 2], axis=AX.X, op=ALU.max, apply_absolute_value=True
             )
 
         def store(j):
@@ -354,10 +361,14 @@ def tile_heterogeneousgraphtransformer_pb_kernel(tc, att, scene_reps, Wo, bo, ga
                 if j > 0:
                     residual(j)
                 stats(j, 0)
+            if 0 <= j - 1 < NT:
+                stats(j - 1, 3)
             if j + 3 < NT:
                 copy_x(j + 3, 0)
             if j < NT:
                 stats(j, 1)
+            if 0 <= j - 1 < NT:
+                hi_on_gpsimd(j - 1, (0,))
             if j + 3 < NT:
                 copy_x(j + 3, 1)
             if j < NT:
@@ -368,19 +379,18 @@ def tile_heterogeneousgraphtransformer_pb_kernel(tc, att, scene_reps, Wo, bo, ga
                 amax(j - 4, j - 4 + 1)
             if 0 <= j - 2 < NT:
                 scale_shift(j - 2)
-            if j - 1 in G_HI_TILES:
-                hi_on_gpsimd(j - 1, (0,))
-            if j - 1 - 1 in G_HI_TILES:
-                hi_on_gpsimd(j - 1 - 1, (2,))
+            if 0 <= j - 2 < NT:
+                hi_on_gpsimd(j - 2, (2,))
             if 5 <= j + 4 < NT:
                 add_bias(j + 4)
-            if j - 1 in G_HI_TILES:
+            if 0 <= j - 1 < NT:
                 hi_on_gpsimd(j - 1, (1,))
             if 0 <= j - 3 < NT:
                 store(j - 3)
             if j + 2 < NT:
                 quantise_x(j + 2)
         amax_before_last()
+        amax_most_of_last_two()
         amax_last()
 
 

@@ -90,13 +90,13 @@ def tile_heterogeneousgraphtransformer_pb_kernel(tc, att, scene_reps, Wo, bo, ga
         load_x(0)
         load_vec(1)
         load_vec(2)
-        load_sr(0)
         nc.sync.dma_start(out=w_raw[0][:], in_=Wo[0 * P : 1 * P, :])
         nc.sync.dma_start(out=w_raw[1][:], in_=Wo[1 * P : 2 * P, :])
         nc.sync.dma_start(out=w_raw[2][:], in_=Wo[2 * P : 3 * P, :])
         nc.sync.dma_start(out=w_raw[3][:], in_=Wo[3 * P : 4 * P, :])
         nc.sync.dma_start(out=w_raw[4][:], in_=Wo[4 * P : 5 * P, :])
         nc.sync.dma_start(out=w_raw[5][:], in_=Wo[5 * P : 6 * P, :])
+        load_sr(0)
         for what, j in LOADS:
             if what == "x":
                 load_x(j)
@@ -126,6 +126,9 @@ def tile_heterogeneousgraphtransformer_pb_kernel(tc, att, scene_reps, Wo, bo, ga
             nc.tensor.matmul(bet_ps[:], lhsT=ones[:], rhs=vec_rows[2][:, 0:LO], start=True, stop=True)
             nc.scalar.copy(out=g_hi[:], in_=bc3[:, 0:HIW])
             nc.scalar.copy(out=b_hi[:], in_=bc4[:, 0:HIW])
+
+        def keep_clock():
+            nc.tensor.matmul(gam_ps[:], lhsT=ones[:], rhs=vec_rows[1][:, 0:LO], start=True, stop=True)
 
         srb = []
         for j in range(NT):
@@ -348,6 +351,8 @@ def tile_heterogeneousgraphtransformer_pb_kernel(tc, att, scene_reps, Wo, bo, ga
         turn_x(2)
         copy_x(2, 0)
         copy_x(2, 1)
+        keep_clock()
+        keep_clock()
         add_bias(2)
         add_bias(3)
         add_bias(4)

@@ -86,17 +86,17 @@ def tile_heterogeneousgraphtransformer_pb_kernel(tc, att, scene_reps, Wo, bo, ga
         def load_sr(j):
             nc.sync.dma_start(out=sr[j][:], in_=sr_v[j])
 
-        load_vec(0)
         load_x(0)
-        load_vec(1)
-        load_vec(2)
         nc.sync.dma_start(out=w_raw[0][:], in_=Wo[0 * P : 1 * P, :])
         nc.sync.dma_start(out=w_raw[1][:], in_=Wo[1 * P : 2 * P, :])
+        load_vec(0)
         nc.sync.dma_start(out=w_raw[2][:], in_=Wo[2 * P : 3 * P, :])
         nc.sync.dma_start(out=w_raw[3][:], in_=Wo[3 * P : 4 * P, :])
         nc.sync.dma_start(out=w_raw[4][:], in_=Wo[4 * P : 5 * P, :])
         nc.sync.dma_start(out=w_raw[5][:], in_=Wo[5 * P : 6 * P, :])
         load_sr(0)
+        load_vec(1)
+        load_vec(2)
         for what, j in LOADS:
             if what == "x":
                 load_x(j)
@@ -122,13 +122,12 @@ def tile_heterogeneousgraphtransformer_pb_kernel(tc, att, scene_reps, Wo, bo, ga
             bc4 = ps.tile([P, 512], F32, tag="bank", name="bc4")
             nc.tensor.matmul(bc3[:, 0:HIW], lhsT=ones[:], rhs=vec_rows[1][:, CS:D], start=True, stop=True)
             nc.tensor.matmul(bc4[:, 0:HIW], lhsT=ones[:], rhs=vec_rows[2][:, CS:D], start=True, stop=True)
-            nc.tensor.matmul(gam_ps[:], lhsT=ones[:], rhs=vec_rows[1][:, 0:LO], start=True, stop=True)
-            nc.tensor.matmul(bet_ps[:], lhsT=ones[:], rhs=vec_rows[2][:, 0:LO], start=True, stop=True)
             nc.scalar.copy(out=g_hi[:], in_=bc3[:, 0:HIW])
             nc.scalar.copy(out=b_hi[:], in_=bc4[:, 0:HIW])
 
-        def keep_clock():
+        def spread_gamma_beta_lo():
             nc.tensor.matmul(gam_ps[:], lhsT=ones[:], rhs=vec_rows[1][:, 0:LO], start=True, stop=True)
+            nc.tensor.matmul(bet_ps[:], lhsT=ones[:], rhs=vec_rows[2][:, 0:LO], start=True, stop=True)
 
         srb = []
         for j in range(NT):
@@ -323,16 +322,15 @@ def tile_heterogeneousgraphtransformer_pb_kernel(tc, att, scene_reps, Wo, bo, ga
         def store(j):
             nc.sync.dma_start(out=out0_v[j], in_=o_all[:, j, :])
 
-        spread_bo()
-        spread_gamma_beta()
         turn_x(0)
         copy_x(0, 0)
         copy_x(0, 1)
         quantise_x(0)
-        add_bias(0)
         turn_w(0)
         copy_w(0)
         quantise_w(0)
+        spread_bo()
+        add_bias(0)
         turn_w(1)
         copy_w(1)
         quantise_w(1)
@@ -351,8 +349,7 @@ def tile_heterogeneousgraphtransformer_pb_kernel(tc, att, scene_reps, Wo, bo, ga
         turn_x(2)
         copy_x(2, 0)
         copy_x(2, 1)
-        keep_clock()
-        keep_clock()
+        spread_gamma_beta_lo()
         add_bias(2)
         add_bias(3)
         add_bias(4)
@@ -394,6 +391,8 @@ def tile_heterogeneousgraphtransformer_pb_kernel(tc, att, scene_reps, Wo, bo, ga
                 store(j - 3)
             if j + 2 < NT:
                 quantise_x(j + 2)
+            if j == 0:
+                spread_gamma_beta()
         amax_before_last()
         amax_most_of_last_two()
         amax_last()

@@ -371,12 +371,12 @@ def tile_heterogeneousgraphtransformer_pb_kernel(tc, att, scene_reps, Wo, bo, ga
                 stats(j, 1)
             if 0 <= j - 1 < NT:
                 hi_on_gpsimd(j - 1, (0,))
+            if 0 <= j - 1 < NT:
+                centre(j - 1)
             if j + 3 < NT:
                 copy_x(j + 3, 1)
             if j < NT:
                 stats(j, 2)
-            if 0 <= j - 1 < NT:
-                centre(j - 1)
             if 0 <= j - 4 < NT - 2:
                 amax(j - 4, j - 4 + 1)
             if 0 <= j - 2 < NT:

@@ -93,7 +93,8 @@ def tile_heterogeneousgraphtransformer_pb_kernel(tc, att, scene_reps, Wo, bo, ga
         nc.sync.dma_start(out=w_raw[2][:], in_=Wo[2 * P : 3 * P, :])
         nc.sync.dma_start(out=w_raw[3][:], in_=Wo[3 * P : 4 * P, :])
         nc.sync.dma_start(out=w_raw[4][:], in_=Wo[4 * P : 5 * P, :])
-        nc.sync.dma_start(out=w_raw[5][:], in_=Wo[5 * P : 6 * P, :])
+        for g in range(NG):
+            nc.sync.dma_start(out=w_raw[5][:, 512 * g : 512 * (g + 1)], in_=Wo[5 * P : 6 * P, 512 * g : 512 * (g + 1)])
         load_sr(0)
         load_vec(1)
         load_vec(2)

from contextlib import ExitStack

import concourse.mybir as mybir
from concourse.masks import make_identity

F32 = mybir.dt.float32
BF16 = mybir.dt.bfloat16
U32 = mybir.dt.uint32
U8 = mybir.dt.uint8
FP8X4 = mybir.dt.float8_e4m3fn_x4
FP8 = mybir.dt.float8_e4m3fn
ALU = mybir.AluOpType
ACT = mybir.ActivationFunctionType
AX = mybir.AxisListType

P = 128
S = 1024
D = 768
E = 2
K = E * D
NT = S // P
NC = 3
CW = D // NC
NG = K // 512
LO = 512
HI = D - LO
EPS = 1e-5

FLOPS = 2 * S * K * D

HIW = 320
CS = D - HIW
V_WEIGHT_BANKS = (1, 4, 7)
V_COPY_TILES = (3, 4, 5,)
LOADS = (("s", 1), ("x", 1), ("x", 2), ("s", 2), ("x", 3), ("x", 4), ("s", 3), ("x", 5), ("x", 6), ("s", 4), ("x", 7), ("s", 5), ("s", 6), ("s", 7))
CASTS = (("v", 0, 1536), ("s", 4096, 5120), ("v", 1536, 3072), ("s", 5120, 6144), ("v", 3072, 4096))


def tile_heterogeneousgraphtransformer_pb_kernel(tc, att, scene_reps, Wo, bo, gamma, beta, out_0, out_1):
    nc = tc.nc
    att_v = att[:, 0, :, :].rearrange("e (p j) d -> j p e d", j=NT)
    sr_v = scene_reps[0, :, :].rearrange("(p j) d -> j p d", j=NT)
    out0_v = out_0[0, :, :].rearrange("(p j) d -> j p d", j=NT)
    out1_v = out_1[0, :, :].rearrange("(p j) d -> p (j d)", j=NT)

    with ExitStack() as ctx:
        const = ctx.enter_context(tc.tile_pool(name="const", bufs=1))
        keep = ctx.enter_context(tc.tile_pool(name="keep", bufs=1))
        work = ctx.enter_context(tc.tile_pool(name="work", bufs=3))
        ps_gb = ctx.enter_context(tc.psum_pool(name="ps_gb", bufs=1))
        ps = ctx.enter_context(tc.psum_pool(name="ps", bufs=6))
        ctx.enter_context(tc.manual_schedule())

        zero_t = const.tile([P, 1], F32, name="zero_t")
        nc.vector.memset(zero_t[:], 0.0)
        eps_t = const.tile([P, 1], F32, name="eps_t")
        nc.vector.tensor_scalar(out=eps_t[:], in0=zero_t[:], scalar1=EPS, scalar2=None, op0=ALU.add)
        warm = const.tile([P, 1], F32, name="warm")
        nc.scalar.activation(out=warm[:], in_=eps_t[:], func=ACT.Abs_reciprocal_sqrt)

        vec_rows = []
        for i in range(3):
            vec_rows.append(const.tile([P, D], BF16, name="vec_row%d" % i))
            nc.gpsimd.memset(vec_rows[i][:].bitcast(F32), 0.0)

        def load_vec(i):
            nc.sync.dma_start(out=vec_rows[i][0:1, :], in_=(bo, gamma, beta)[i].rearrange("(o d) -> o d", o=1))

        ones = const.tile([P, P], BF16, name="ones")
        nc.vector.memset(ones[:], 1.0)
        ident = const.tile([P, P], F32, name="ident")
        make_identity(nc, ident[:])

        w_raw = []
        x_raw = []
        sr = []
        for r in range(2 * NC):
            w_raw.append(keep.tile([P, K], BF16, name="w_raw%d" % r))
        for j in range(NT):
            x_raw.append(keep.tile([P, K], BF16, name="x_raw%d" % j))
            sr.append(keep.tile([P, D], BF16, name="sr%d" % j))

        def load_x(j):
            nc.sync.dma_start(out=x_raw[j][:].rearrange("p (e d) -> p e d", e=E), in_=att_v[j])

        def load_sr(j):
            nc.sync.dma_start(out=sr[j][:], in_=sr_v[j])

        load_x(0)
        nc.sync.dma_start(out=w_raw[0][:], in_=Wo[0 * P : 1 * P, :])
        nc.sync.dma_start(out=w_raw[1][:], in_=Wo[1 * P : 2 * P, :])
        load_vec(0)
        nc.sync.dma_start(out=w_raw[2][:], in_=Wo[2 * P : 3 * P, :])
        nc.sync.dma_start(out=w_raw[3][:], in_=Wo[3 * P : 4 * P, :])
        nc.sync.dma_start(out=w_raw[4][:], in_=Wo[4 * P : 5 * P, :])
        for g in range(NG):
            nc.sync.dma_start(out=w_raw[5][:, 512 * g : 512 * (g + 1)], in_=Wo[5 * P : 6 * P, 512 * g : 512 * (g + 1)])
        load_sr(0)
        load_vec(1)
        load_vec(2)
        for what, j in LOADS:
            if what == "x":
                load_x(j)
            else:
                load_sr(j)

        gam_ps = ps_gb.tile([P, LO], F32, name="gam_ps")
        bet_ps = ps_gb.tile([P, LO], F32, name="bet_ps")
        bo_sb = const.tile([P, D], BF16, name="bo_sb")
        g_hi = const.tile([P, HIW], F32, name="g_hi")
        b_hi = const.tile([P, HIW], F32, name="b_hi")

        def spread_bo():
            bc1 = ps.tile([P, 512], F32, tag="bank", name="bc1")
            bc2 = ps.tile([P, 512], F32, tag="bank", name="bc2")
            nc.tensor.matmul(bc1[:], lhsT=ones[:], rhs=vec_rows[0][:, 0:LO], start=True, stop=True)
            nc.tensor.matmul(bc2[:, 0:HI], lhsT=ones[:], rhs=vec_rows[0][:, LO:D], start=True, stop=True)
            nc.scalar.copy(out=bo_sb[:, 0:LO], in_=bc1[:])
            nc.scalar.copy(out=bo_sb[:, LO:D], in_=bc2[:, 0:HI])

        def spread_gamma_beta():
            bc3 = ps.tile([P, 512], F32, tag="bank", name="bc3")
            bc4 = ps.tile([P, 512], F32, tag="bank", name="bc4")
            nc.tensor.matmul(bc3[:, 0:HIW], lhsT=ones[:], rhs=vec_rows[1][:, CS:D], start=True, stop=True)
            nc.tensor.matmul(bc4[:, 0:HIW], lhsT=ones[:], rhs=vec_rows[2][:, CS:D], start=True, stop=True)
            nc.scalar.copy(out=g_hi[:], in_=bc3[:, 0:HIW])
            nc.scalar.copy(out=b_hi[:], in_=bc4[:, 0:HIW])

        def spread_gamma_beta_lo():
            nc.tensor.matmul(gam_ps[:], lhsT=ones[:], rhs=vec_rows[1][:, 0:LO], start=True, stop=True)
            nc.tensor.matmul(bet_ps[:], lhsT=ones[:], rhs=vec_rows[2][:, 0:LO], start=True, stop=True)

        srb = []
        for j in range(NT):
            srb.append(keep.tile([P, D], F32, name="srb%d" % j))
        o_ext = keep.tile([P, NT * D + 2], F32, name="o_ext")
        o_all = o_ext[:, 0 : NT * D].rearrange("p (j d) -> p j d", j=NT)
        negmu = const.tile([P, NT], F32, name="negmu")
        ssq = const.tile([P, NT], F32, name="ssq")
        rstd = const.tile([P, NT], F32, name="rstd")
        pm = const.tile([P, NT], F32, name="pm")
        nmr = const.tile([P, NT], F32, name="nmr")

        def turn(dst_bank, slot, words, g):
            for u in range(2):
                nc.tensor.transpose(dst_bank[:, slot, u, :], words[:, 256 * g + u : 256 * (g + 1) : 2], ident[:])

        w_banks = {}
        w_grouped = {}
        wq = {}

        def turn_w(c):
            banks = []
            for g in range(NG):
                banks.append(ps.tile([P, 2, 2, P], F32, tag="bank", name="wt_%d_%d" % (c, g)))
            for tl in range(2):
                for g in range(NG):
                    turn(banks[g], tl, w_raw[2 * c + tl][:].bitcast(F32), g)
            w_banks[c] = banks

        def copy_w(c):
            grouped = keep.tile([P, NG * 1024], BF16, name="grp_w%d" % c, align_bytes=64)
            g32 = grouped[:].bitcast(F32).rearrange("p (g t r u) -> p g t r u", g=NG, t=2, u=2)
            for g in range(NG):
                src = w_banks[c][g][:].rearrange("p t u r -> p t r u")
                if (c * NG + g) in V_WEIGHT_BANKS:
                    nc.vector.tensor_copy(out=g32[:, g], in_=src)
                else:
                    nc.scalar.copy(out=g32[:, g], in_=src)
            w_grouped[c] = grouped

        def quantise_w(c):
            grouped = w_grouped[c]
            codes = keep.tile([P, NG * 256], U32, name="c_w%d" % c, align_bytes=64)
            scales = keep.tile([P, NG * 256], U8, name="s_w%d" % c, align_bytes=64)
            nc.vector.quantize_mx(out=codes[:, 0:512].bitcast(FP8X4), scales=scales[:, 0:512], in_=grouped[:, 0:2048])
            nc.vector.quantize_mx(out=codes[:, 512:768].bitcast(FP8X4), scales=scales[:, 512:768], in_=grouped[:, 2048:3072])
            wq[c] = (codes, scales)

        x_banks = {}
        x_grouped = {}
        xq = {}

        def turn_x(j):
            words = x_raw[j][:].bitcast(F32)
            xa = ps.tile([P, 2, 2, P], F32, tag="bank", name="xa_%d" % j)
            xb = ps.tile([P, 2, 2, P], F32, tag="bank", name="xb_%d" % j)
            turn(xa, 0, words, 0)
            turn(xa, 1, words, 1)
            turn(xb, 0, words, 2)
            x_banks[j] = (xa, xb)

        def copy_x(j, part):
            if j not in x_grouped:
                x_grouped[j] = keep.tile([P, NG * 512], BF16, name="grp_x%d" % j, align_bytes=64)
            g32 = x_grouped[j][:].bitcast(F32).rearrange("p (g r u) -> p g r u", g=NG, u=2)
            if part == 0:
                nc.scalar.copy(out=g32[:, 0:2], in_=x_banks[j][0][:].rearrange("p g u r -> p g r u"))
            elif j in V_COPY_TILES:
                nc.vector.tensor_copy(out=g32[:, 2:3], in_=x_banks[j][1][:, 0:1].rearrange("p g u r -> p g r u"))
            else:
                nc.scalar.copy(out=g32[:, 2:3], in_=x_banks[j][1][:, 0:1].rearrange("p g u r -> p g r u"))

        def quantise_x(j):
            grouped = x_grouped[j]
            codes = keep.tile([P, NG * P], U32, name="c_x%d" % j, align_bytes=64)
            scales = keep.tile([P, NG * P], U8, name="s_x%d" % j, align_bytes=64)
            nc.vector.quantize_mx(out=codes[:, 0:256].bitcast(FP8X4), scales=scales[:, 0:256], in_=grouped[:, 0:1024])
            nc.vector.quantize_mx(out=codes[:, 256:384].bitcast(FP8X4), scales=scales[:, 256:384], in_=grouped[:, 1024:1536])
            xq[j] = (codes, scales)

        def add_bias(j):
            nc.gpsimd.tensor_tensor(out=srb[j][:], in0=sr[j][:], in1=bo_sb[:], op=ALU.add)

        accs = {}

        def multiply(j, chunks):
            codes, scales = xq[j]
            if j not in accs:
                acc_lo = ps.tile([P, 512], F32, tag="bank", name="acc_lo")
                acc_hi = ps.tile([P, 512], F32, tag="bank", name="acc_hi")
                accs[j] = (acc_lo, acc_hi)
            acc_lo, acc_hi = accs[j]
            outs = (acc_lo[:, 0:CW], acc_lo[:, CW : 2 * CW], acc_hi[:, 0:CW])
            for c in chunks:
                for g in range(NG):
                    cols = slice(g * P, (g + 1) * P)
                    nc.tensor.matmul_mx(
                        out=outs[c],
                        lhsT=codes[:, cols].bitcast(FP8X4),
                        lhsT_scale=scales[:, cols],
                        rhs=wq[c][0][:, g * CW : (g + 1) * CW].bitcast(FP8X4),
                        rhs_scale=wq[c][1][:, g * CW : (g + 1) * CW],
                        start=(g == 0),
                        stop=(g == NG - 1),
                    )

        ys = {}

        def residual(j, parts=(0, 1)):
            acc_lo, acc_hi = accs[j]
            if j not in ys:
                ys[j] = work.tile([P, D], F32, tag="y", name="y", bufs=5)
            y = ys[j]
            if 0 in parts:
                nc.vector.tensor_tensor(out=y[:, 0:LO], in0=acc_lo[:, 0:LO], in1=srb[j][:, 0:LO], op=ALU.add)
            if 1 in parts:
                nc.vector.tensor_tensor(out=y[:, LO:D], in0=acc_hi[:, 0:HI], in1=srb[j][:, LO:D], op=ALU.add)

        def stats(j, part):
            y = ys[j]
            col = slice(j, j + 1)
            if part == 0:
                junk = work.tile([P, D], BF16, tag="junk", name="junk", bufs=2)
                nc.scalar.activation(out=junk[:], in_=y[:], func=ACT.Identity, scale=-1.0 / D, accum_out=negmu[:, col])
            if part == 1:
                junk2 = work.tile([P, D], BF16, tag="junk", name="junk2", bufs=2)
                nc.scalar.activation(out=junk2[:], in_=y[:], func=ACT.Square, bias=negmu[:, col], accum_out=ssq[:, col])
            if part == 2:
                nc.scalar.activation(
                    out=rstd[:, col], in_=ssq[:, col], func=ACT.Abs_reciprocal_sqrt, bias=eps_t[:, 0:1], scale=1.0 / D
                )
            if part == 3:
                nc.scalar.activation(out=nmr[:, col], in_=negmu[:, col], func=ACT.Copy, scale=rstd[:, col])

        ts = {}

        def centre(j):
            y = ys[j]
            col = slice(j, j + 1)
            t = work.tile([P, D], F32, tag="t", name="t", bufs=4)
            ts[j] = t
            nc.vector.scalar_tensor_tensor(
                out=t[:, 0:CS], in0=y[:, 0:CS], scalar=negmu[:, col], in1=gam_ps[:, 0:CS], op0=ALU.add, op1=ALU.mult
            )

        def scale_shift(j):
            t = ts[j]
            col = slice(j, j + 1)
            nc.vector.scalar_tensor_tensor(
                out=o_all[:, j, 0:CS], in0=t[:, 0:CS], scalar=rstd[:, col], in1=bet_ps[:, 0:CS], op0=ALU.mult, op1=ALU.add
            )

        zs = {}

        def hi_on_gpsimd(j, parts=(0, 1, 2)):
            y = ys[j]
            col = slice(j, j + 1)
            if j not in zs:
                zs[j] = work.tile([P, HIW], F32, tag="z", name="z", bufs=3)
            z = zs[j]
            if 0 in parts:
                nc.scalar.activation(out=z[:], in_=y[:, CS:D], func=ACT.Identity, scale=rstd[:, col], bias=nmr[:, col])
            if 1 in parts:
                nc.gpsimd.tensor_tensor(out=z[:], in0=z[:], in1=g_hi[:], op=ALU.mult)
            if 2 in parts:
                nc.gpsimd.tensor_tensor(out=o_all[:, j, CS:D], in0=z[:], in1=b_hi[:], op=ALU.add)

        def amax(j0, j1):
            nc.vector.tensor_reduce(
                out=pm[:, j0:j1], in_=o_all[:, j0:j1, :], axis=AX.X, op=ALU.max, apply_absolute_value=True
            )

        pmax = const.tile([P, 1], F32, name="pmax")

        def amax_before_last():
            nc.vector.tensor_reduce(out=o_ext[:, NT * D : NT * D + 1], in_=pm[:, 0 : NT - 2], axis=AX.X, op=ALU.max)

        def amax_most_of_last_two():
            nc.vector.tensor_reduce(
                out=o_ext[:, NT * D + 1 : NT * D + 2],
                in_=o_ext[:, (NT - 2) * D : (NT - 1) * D + CS],
                axis=AX.X,
                op=ALU.max,
                apply_absolute_value=True,
            )

        def amax_last():
            nc.vector.tensor_reduce(
                out=pmax[:], in_=o_ext[:, (NT - 1) * D + CS : NT * D + 2], axis=AX.X, op=ALU.max, apply_absolute_value=True
            )

        def store(j):
            nc.sync.dma_start(out=out0_v[j], in_=o_all[:, j, :])

        turn_x(0)
        copy_x(0, 0)
        copy_x(0, 1)
        quantise_x(0)
        turn_w(0)
        copy_w(0)
        quantise_w(0)
        spread_bo()
        add_bias(0)
        turn_w(1)
        copy_w(1)
        quantise_w(1)
        turn_w(2)
        copy_w(2)
        quantise_w(2)
        add_bias(1)
        multiply(0, (0, 1))
        turn_x(1)
        copy_x(1, 0)
        copy_x(1, 1)
        multiply(0, (2,))
        residual(0, (0,))
        quantise_x(1)
        residual(0, (1,))
        turn_x(2)
        copy_x(2, 0)
        copy_x(2, 1)
        spread_gamma_beta_lo()
        add_bias(2)
        add_bias(3)
        add_bias(4)

        for j in range(NT + 4):
            if j + 3 < NT:
                turn_x(j + 3)
            if j + 1 < NT:
                multiply(j + 1, (0, 1, 2))
            if j < NT:
                if j > 0:
                    residual(j)
                stats(j, 0)
            if 0 <= j - 1 < NT:
                stats(j - 1, 3)
            if j + 3 < NT:
                copy_x(j + 3, 0)
            if j < NT:
                stats(j, 1)
            if 0 <= j - 1 < NT:
                hi_on_gpsimd(j - 1, (0,))
            if 0 <= j - 1 < NT:
                centre(j - 1)
            if j + 3 < NT:
                copy_x(j + 3, 1)
            if j < NT:
                stats(j, 2)
            if 0 <= j - 4 < NT - 2:
                amax(j - 4, j - 4 + 1)
            if 0 <= j - 2 < NT:
                scale_shift(j - 2)
            if 0 <= j - 2 < NT:
                hi_on_gpsimd(j - 2, (2,))
            if 5 <= j + 4 < NT:
                add_bias(j + 4)
            if 0 <= j - 1 < NT:
                hi_on_gpsimd(j - 1, (1,))
            if 0 <= j - 3 < NT:
                store(j - 3)
            if j + 2 < NT:
                quantise_x(j + 2)
            if j == 0:
                spread_gamma_beta()
        amax_before_last()
        amax_most_of_last_two()
        amax_last()


        tp = ps.tile([P, 512], F32, tag="bank", name="tp")
        nc.tensor.transpose(tp[:, 0:P], pmax[:, 0:1].to_broadcast([P, P]), ident[:])
        scaled = const.tile([P, P], F32, name="scaled")
        s_t = const.tile([P, 1], F32, name="s_t")
        nc.vector.tensor_scalar(out=scaled[:], in0=tp[:, 0:P], scalar1=1.0 / 448.0, scalar2=None, op0=ALU.mult, op1=ALU.max, accum_out=s_t[:])
        fac = const.tile([P, 1], F32, name="fac")
        nc.vector.reciprocal(out=fac[:], in_=s_t[:])

        o_flat = o_ext[:, 0 : NT * D]
        for i, (eng, c0, c1) in enumerate(CASTS):
            q = keep.tile([P, c1 - c0], FP8, name="q%d" % i)
            if eng == "v":
                nc.vector.tensor_scalar(
                    out=q[:], in0=o_flat[:, c0:c1], scalar1=fac[:, 0:1], scalar2=None, op0=ALU.mult, saturate=False
                )
            else:
                nc.scalar.activation(
                    out=q[:], in_=o_flat[:, c0:c1], func=ACT.Identity, scale=fac[:, 0:1], bias=zero_t[:, 0:1], saturate=False
                )
            nc.sync.dma_start(out=out1_v[:, c0:c1], in_=q[:].bitcast(U8))
